import numpy as np
import ml_dtypes


def mxq(x, axis, fmt="e4m3"):
    dtype, down = {"e4m3": (ml_dtypes.float8_e4m3fn, 7), "e5m2": (ml_dtypes.float8_e5m2, 14)}[fmt]
    v = np.moveaxis(np.asarray(x, np.float32).astype(ml_dtypes.bfloat16).astype(np.float64), axis, -1)
    blocks = v.reshape(v.shape[:-1] + (-1, 32))
    amax = np.abs(blocks).max(-1, keepdims=True)
    byte = np.maximum(np.where(amax > 0, np.frexp(amax)[1] - 1 + 127, 0) - down, 1)
    scale = np.exp2(byte - 127.0)
    codes = (blocks / scale).astype(np.float32).astype(dtype).astype(np.float64)
    return np.moveaxis((codes * scale).reshape(v.shape), -1, axis)


WIDE = False


def mx_kscale(k):
    if not WIDE:
        return np.ones(k)
    levels = np.array([10, -10, 5, -5, 0])
    a = np.random.permutation(np.resize(levels, k // 512 * 4)).reshape(k // 512, 4)
    idx = np.arange(k)
    return np.exp2(a[idx // 512, idx % 128 // 32])


BF16 = ml_dtypes.bfloat16


def bf(x):
    return np.asarray(x, np.float32).astype(BF16)


def f64(x):
    return np.asarray(x).astype(np.float64)


B, H = 512, 1024
K = 2 * H
G = 4 * H


def sigmoid(v):
    return 1.0 / (1.0 + np.exp(-v))


def setup_inputs():
    s = mx_kscale(K)
    return {"x": bf(np.random.standard_normal((B, H)) * s[:H]),
            "h_prev": bf(np.random.standard_normal((B, H)) * s[H:]),
            "c_prev": bf(np.random.standard_normal((B, H))),
            "is_rnn": bf(np.random.random((B, 1))),
            "W": bf(np.random.standard_normal((K, G)) / np.sqrt(K) / s[:, None]),
            "b": bf(np.random.standard_normal(G) * 0.3)}


def reference(x, h_prev, c_prev, is_rnn, W, b):
    c_prev, m = f64(c_prev), f64(is_rnn)
    xh = np.concatenate([f64(x), f64(h_prev)], axis=1)
    gates = (mxq(xh, 1, "e4m3") @ mxq(f64(W), 0, "e4m3")) + f64(b)
    i = sigmoid(gates[:, :H])
    f = sigmoid(gates[:, H:2 * H])
    g = np.tanh(gates[:, 2 * H:3 * H])
    o = sigmoid(gates[:, 3 * H:])
    c = f * c_prev + i * g
    c = c * m + c_prev * (1.0 - m)
    o = o * m + (1.0 - m)
    return c, o

@@ -1,0 +1,346 @@
+from contextlib import ExitStack
+
+import concourse.mybir as mybir
+from concourse.masks import make_identity
+
+F32 = mybir.dt.float32
+BF16 = mybir.dt.bfloat16
+U32 = mybir.dt.uint32
+U8 = mybir.dt.uint8
+FP8X4 = mybir.dt.float8_e4m3fn_x4
+ACT = mybir.ActivationFunctionType
+ALU = mybir.AluOpType
+
+P = 128
+B = 512
+H = 1024
+K = 2 * H
+G = 4 * H
+FLOPS = 2 * B * K * G
+
+NBT = B // P
+HALF = 512
+ROLES = "gfio"
+BLOCK = {"i": 0, "f": 1, "g": 2, "o": 3}
+NP = 32
+N_RAW = 22
+CP_BEFORE = 16
+BIAS_SLOT = 4
+LAG_A = 3
+SLOTS = {"A6": 29, "To0": 30, "o0": 31, "ig1": 32, "Tig1": 33, "c1": 33, "A7": 33,
+         "fb0": 17, "u0": 18, "fb1": 21, "u1": 22}
+MM_FIRST = (30, 31, 32, 33)
+SHARES = (336, 160, 152, 152, 152, 248, 512, 360, 248, 240, 512, 360, 248, 248, 512, 360,
+          240, 512, 376, 248, 248, 512, 376, 0, 128, 0, 512, 232, 248, 512, 352, 512)
+
+
+def tile_bag_lstm_pa_kernel(tc, x, h_prev, c_prev, is_rnn, W, b, out_0, out_1):
+    nc = tc.nc
+    with ExitStack() as ctx:
+        const = ctx.enter_context(tc.tile_pool(name="const", bufs=1))
+        rawp = ctx.enter_context(tc.tile_pool(name="rawp", bufs=N_RAW))
+        grpp = ctx.enter_context(tc.tile_pool(name="grpp", bufs=4))
+        codep = ctx.enter_context(tc.tile_pool(name="codep", bufs=8))
+        keepp = ctx.enter_context(tc.tile_pool(name="keepp", bufs=2))
+        actp = ctx.enter_context(tc.tile_pool(name="actp", bufs=3))
+        fpp = ctx.enter_context(tc.tile_pool(name="fpp", bufs=2))
+        ostp = ctx.enter_context(tc.tile_pool(name="ostp", bufs=10))
+        mxps = ctx.enter_context(tc.psum_pool(name="mxps", bufs=4))
+        tpps = ctx.enter_context(tc.psum_pool(name="tpps", bufs=4))
+        ctx.enter_context(tc.manual_schedule())
+
+        state = {"issued": 0, "released": 0, "act_units": 0, "quantised": 0, "multiplied": 0}
+
+        warm = const.tile([P, 1], F32, name="warm", tag="warm")
+        warm2 = const.tile([P, 1], F32, name="warm2", tag="warm2")
+        nc.vector.memset(warm[:], 0.0)
+        bm_raw = const.tile([P, P], BF16, name="bm_raw", tag="bm_raw")
+        nc.vector.memset(bm_raw[:], 0.0)
+        nc.scalar.dma_start(out=bm_raw[0:32, :], in_=b.rearrange("(r c) -> r c", c=P))
+        nc.scalar.dma_start(out=bm_raw[32:36, :], in_=is_rnn.rearrange("(r p) o -> r (p o)", p=P))
+        nc.scalar.activation(out=warm2[:], in_=warm[:], func=ACT.Sigmoid)
+        ident = const.tile([P, P], F32, name="ident", tag="ident")
+        make_identity(nc, ident[:])
+
+        raws = {}
+        xraws = {}
+        cp_sb = const.tile([P, NBT * H], BF16, name="cp_sb", tag="cp_sb")
+
+        def load_w(n):
+            unit, p = divmod(n, 4)
+            gi, half = divmod(unit, 2)
+            col0 = BLOCK[ROLES[gi]] * H + half * HALF
+            rt = rawp.tile([P, 4 * HALF], BF16, name="raw", tag="raw")
+            raws[n] = rt[:].rearrange("p (t c) -> p t c", t=4)
+            for u in range(2):
+                r0 = 512 * p + 256 * u
+                nc.sync.dma_start(
+                    out=raws[n][:, 2 * u : 2 * u + 2, :],
+                    in_=W[r0 : r0 + 256, col0 : col0 + HALF].rearrange("(q e) c -> q e c", e=2),
+                )
+
+        def load_x(p):
+            src = x if p < 2 else h_prev
+            c0 = (p % 2) * 512
+            xt = rawp.tile([P, NBT * 512], BF16, name="xraw", tag="raw")
+            xraws[p] = xt
+            nc.sync.dma_start(
+                out=xt[:].rearrange("p (t c) -> p t c", t=NBT),
+                in_=src[:, c0 : c0 + 512].rearrange("(t p) c -> p t c", p=P),
+            )
+
+        def load_cp():
+            nc.sync.dma_start(
+                out=cp_sb[:].rearrange("p (t c) -> p t c", t=NBT),
+                in_=c_prev.rearrange("(t p) c -> p t c", p=P),
+            )
+
+        loads = []
+        for n in range(NP):
+            loads.append(("w", n))
+            if n < 4:
+                loads.append(("x", n))
+
+        def pump():
+            while state["issued"] < len(loads) and state["issued"] - state["released"] < N_RAW:
+                kind, n = loads[state["issued"]]
+                if kind == "w":
+                    if n == CP_BEFORE:
+                        load_cp()
+                    load_w(n)
+                else:
+                    load_x(n)
+                state["issued"] += 1
+
+        pump()
+
+        bmT = const.tile([P, 36], F32, name="bmT", tag="bmT")
+        om = const.tile([P, NBT], F32, name="om", tag="om")
+
+        def prep_bias():
+            bm_f = const.tile([P, P], F32, name="bm_f", tag="bm_f")
+            nc.vector.tensor_copy(out=bm_f[:], in_=bm_raw[:])
+            bm_ps = tpps.tile([P, 512], F32, name="bm_ps", tag="tp")
+            nc.tensor.transpose(bm_ps[:, 0:P], bm_f[:], ident[:])
+            nc.vector.tensor_copy(out=bmT[:], in_=bm_ps[:, 0:36])
+            nc.vector.tensor_scalar(
+                out=om[:], in0=bmT[:, 32:36], scalar1=-1.0, scalar2=1.0, op0=ALU.mult, op1=ALU.add
+            )
+
+        def m_col(bt):
+            return bmT[:, 32 + bt : 33 + bt]
+
+        xcodes = const.tile([P, 4 * B], U32, name="xcodes", tag="xcodes", align_bytes=64)
+        xplane = const.tile([P, 4 * B], U8, name="xplane", tag="xplane", align_bytes=64)
+        xgs = {}
+
+        def xcopy(p):
+            s32 = xraws[p][:].bitcast(F32)
+            xg = grpp.tile([P, 4 * B], BF16, name="xg", tag="grp", align_bytes=64)
+            xgs[p] = xg
+            xg32 = xg[:].bitcast(F32).rearrange("p (n u) -> p n u", u=2)
+            for bp in range(2):
+                xt = tpps.tile([P, 512], F32, name="xt", tag="tp")
+                xtv = xt[:].rearrange("p (u n) -> p u n", u=2)
+                for u in range(2):
+                    for b2 in range(2):
+                        w0 = (2 * bp + b2) * 256 + u * P
+                        nc.tensor.transpose(
+                            xtv[:, u, b2 * P : (b2 + 1) * P], s32[:, w0 : w0 + P], ident[:]
+                        )
+                dst = xg32[:, bp * 256 : (bp + 1) * 256, :]
+                srcv = xt[:].rearrange("p (u n) -> p n u", u=2)
+                if bp == 0:
+                    nc.vector.tensor_copy(out=dst, in_=srcv)
+                else:
+                    nc.scalar.copy(out=dst, in_=srcv)
+            state["released"] += 1
+            pump()
+
+        def xquant(p):
+            nc.vector.quantize_mx(
+                out=xcodes[:, p * B : (p + 1) * B].bitcast(FP8X4),
+                scales=xplane[:, p * B : (p + 1) * B],
+                in_=xgs[p][:],
+            )
+
+        grps = {}
+        codes = {}
+        banks = {}
+        keep = {}
+        acts = {}
+        fps = {}
+        tbs = {}
+
+        def regroup(n):
+            rv = raws[n]
+            grp = grpp.tile([P, 4 * HALF], BF16, name="grp", tag="grp", align_bytes=64)
+            grps[n] = grp
+            gv = grp[:].rearrange("p (c t) -> p c t", t=4)
+            a = SHARES[n]
+            if a > 0:
+                nc.vector.tensor_copy(
+                    out=gv[:, 0:a, :].rearrange("p (c i) t -> p c t i", i=4),
+                    in_=rv[:, :, 0:a].rearrange("p t (c i) -> p c t i", i=4),
+                )
+            if a < HALF:
+                nc.scalar.copy(
+                    out=gv[:, a:HALF, :].rearrange("p (c i) t -> p c t i", i=4),
+                    in_=rv[:, :, a:HALF].rearrange("p t (c i) -> p c t i", i=4),
+                )
+            state["released"] += 1
+            pump()
+
+        def quantise(n):
+            wc = codep.tile([P, HALF], U32, name="wc", tag="wc", align_bytes=64)
+            wp = codep.tile([P, HALF], U8, name="wp", tag="wp", align_bytes=64)
+            nc.vector.quantize_mx(out=wc[:].bitcast(FP8X4), scales=wp[:], in_=grps[n][:])
+            codes[n] = (wc, wp)
+            state["quantised"] += 1
+
+        def matmuls(n):
+            unit, p = divmod(n, 4)
+            wc, wp = codes[n]
+            for jj in range(4):
+                if p == 0:
+                    bank = mxps.tile([P, B], F32, name="bank", tag="mx")
+                    banks[(unit, jj)] = bank
+                nc.tensor.matmul_mx(
+                    out=banks[(unit, jj)][:],
+                    lhsT=wc[:, jj * P : (jj + 1) * P].bitcast(FP8X4),
+                    lhsT_scale=wp[:, jj * P : (jj + 1) * P],
+                    rhs=xcodes[:, p * B : (p + 1) * B].bitcast(FP8X4),
+                    rhs_scale=xplane[:, p * B : (p + 1) * B],
+                    start=(p == 0),
+                    stop=(p == 3),
+                )
+
+        def flush():
+            while state["multiplied"] < state["quantised"] and (
+                state["multiplied"] % 4 != 0 or state["act_units"] >= state["multiplied"] // 4
+            ):
+                matmuls(state["multiplied"])
+                state["multiplied"] += 1
+
+        def activations(unit):
+            gi, half = divmod(unit, 2)
+            role = ROLES[gi]
+            if role == "g":
+                aT = keepp.tile([P, 4, B], F32, name="gT", tag="gT")
+                keep[half] = aT
+            else:
+                aT = actp.tile([P, 4, B], F32, name="aT", tag="aT")
+            acts[unit] = aT
+            for jj in range(4):
+                col = BLOCK[role] * 8 + half * 4 + jj
+                nc.scalar.activation(
+                    out=aT[:, jj, :],
+                    in_=banks[(unit, jj)][:],
+                    func=ACT.Tanh if role == "g" else ACT.Sigmoid,
+                    bias=bmT[:, col : col + 1],
+                    scale=1.0,
+                )
+            state["act_units"] += 1
+
+        def transposes(key, srcT, pool, tag):
+            for bt in range(NBT):
+                tb = pool.tile([P, 512], F32, name="tb", tag=tag)
+                tbs[(key, bt)] = tb
+                for jj in range(4):
+                    nc.tensor.transpose(
+                        tb[:, jj * P : (jj + 1) * P], srcT[:, jj, bt * P : (bt + 1) * P], ident[:]
+                    )
+
+        def blend_scalar(dst, tb, bt):
+            nc.scalar.activation(
+                out=dst, in_=tb[:], func=ACT.Identity, bias=om[:, bt : bt + 1], scale=m_col(bt)
+            )
+
+        def blend_vector(dst, tb, bt):
+            nc.vector.tensor_scalar(
+                out=dst, in0=tb[:], scalar1=m_col(bt), scalar2=om[:, bt : bt + 1],
+                op0=ALU.mult, op1=ALU.add,
+            )
+
+        def mul_ig(half, unit):
+            nc.vector.tensor_tensor(out=keep[half][:], in0=acts[unit][:], in1=keep[half][:], op=ALU.mult)
+
+        def f_blend(half):
+            fp = fpp.tile([P, NBT, HALF], F32, name="fp", tag="fp")
+            fps[half] = fp
+            for bt in range(NBT):
+                blend_scalar(fp[:, bt, :], tbs[(("f", half), bt)], bt)
+
+        def f_times_c(half):
+            cols = slice(half * HALF, (half + 1) * HALF)
+            cpv = cp_sb[:].rearrange("p (t c) -> p t c", t=NBT)[:, :, cols]
+            nc.vector.tensor_tensor(out=fps[half][:], in0=fps[half][:], in1=cpv, op=ALU.mult)
+
+        def c_out(half):
+            cols = slice(half * HALF, (half + 1) * HALF)
+            for bt in range(NBT):
+                cst = ostp.tile([P, HALF], F32, name="cst", tag="ost")
+                nc.vector.scalar_tensor_tensor(
+                    out=cst[:], in0=tbs[(("ig", half), bt)][:], scalar=m_col(bt),
+                    in1=fps[half][:, bt, :], op0=ALU.mult, op1=ALU.add,
+                )
+                nc.sync.dma_start(out=out_0[bt * P : (bt + 1) * P, cols], in_=cst[:])
+
+        def o_out(half, vector_bts):
+            cols = slice(half * HALF, (half + 1) * HALF)
+            for bt in range(NBT):
+                ost = ostp.tile([P, HALF], F32, name="ost", tag="ost")
+                if bt in vector_bts:
+                    blend_vector(ost[:], tbs[(("o", half), bt)], bt)
+                else:
+                    blend_scalar(ost[:], tbs[(("o", half), bt)], bt)
+                nc.sync.dma_start(out=out_1[bt * P : (bt + 1) * P, cols], in_=ost[:])
+
+        tasks = {}
+
+        def at(name, slot, fn):
+            slot = SLOTS.get(name, slot)
+            tasks[slot] = tasks.get(slot, []) + [fn]
+            return slot
+
+        u_slot = {}
+        for unit in range(8):
+            gi, half = divmod(unit, 2)
+            role = ROLES[gi]
+            s_a = at("A%d" % unit, 4 * unit + 3 + LAG_A, lambda unit=unit: activations(unit))
+            if role == "f":
+                at("Tf%d" % half, s_a + 1,
+                   lambda unit=unit, half=half: transposes(("f", half), acts[unit], tpps, "tp"))
+                s_b = at("fb%d" % half, s_a + 2, lambda half=half: f_blend(half))
+                u_slot[half] = at("u%d" % half, s_b + 1, lambda half=half: f_times_c(half))
+            elif role == "o":
+                if unit == 7:
+                    at("To%d" % half, s_a + 1,
+                       lambda unit=unit, half=half: transposes(("o", half), acts[unit], mxps, "mx"))
+                    at("o%d" % half, s_a + 2, lambda half=half: o_out(half, (0, 1)))
+                else:
+                    at("To%d" % half, s_a + 1,
+                       lambda unit=unit, half=half: transposes(("o", half), acts[unit], tpps, "tp"))
+                    at("o%d" % half, s_a + 2, lambda half=half: o_out(half, ()))
+            elif role == "i":
+                s_i = at("ig%d" % half, s_a + 1, lambda unit=unit, half=half: mul_ig(half, unit))
+                s_t = at("Tig%d" % half, max(s_i + 1, u_slot[half]),
+                         lambda half=half: transposes(("ig", half), keep[half], tpps, "tp"))
+                at("c%d" % half, s_t + 1, lambda half=half: c_out(half))
+
+        for s in range(NP + 6):
+            if s < NP:
+                regroup(s)
+            if 1 <= s <= NP:
+                quantise(s - 1)
+            if 1 <= s <= 4:
+                xquant(s - 1)
+            if s < 4:
+                xcopy(s)
+            if s == BIAS_SLOT:
+                prep_bias()
+            if s in MM_FIRST:
+                flush()
+            for fn in tasks.get(s, []):
+                fn()
+            flush()

@@ -15,332 +15,309 @@ P = 128
 B = 512
 H = 1024
 K = 2 * H
-G = 4 * H
-FLOPS = 2 * B * K * G
+FLOPS = 2 * B * K * 4 * H
 
-NBT = B // P
-HALF = 512
-ROLES = "gfio"
+K_PASS = 512
+PASSES = K // K_PASS
+ROW_TILES = B // P
+UNIT = 512
+TILES = UNIT // P
+GATES = "gfio"
 BLOCK = {"i": 0, "f": 1, "g": 2, "o": 3}
-NP = 32
-N_RAW = 22
-CP_BEFORE = 16
-BIAS_SLOT = 4
-LAG_A = 3
-SLOTS = {"A6": 29, "To0": 30, "o0": 31, "ig1": 32, "Tig1": 33, "c1": 33, "A7": 33,
-         "fb0": 17, "u0": 18, "fb1": 21, "u1": 22}
-MM_FIRST = (30, 31, 32, 33)
-SHARES = (336, 160, 152, 152, 152, 248, 512, 360, 248, 240, 512, 360, 248, 248, 512, 360,
-          240, 512, 376, 248, 248, 512, 376, 0, 128, 0, 512, 232, 248, 512, 352, 512)
+UNITS = 2 * len(GATES)
+PIECES = UNITS * PASSES
+
+LAG_ACTIVATE = 3
+LAG_TRANSPOSE = 4
+LAG_F_BLEND = 6
+LAG_F_TIMES_C = 7
+LAG_I_TIMES_G = 9
+LAG_C_OUT = 10
+LAG_O_OUT = 5
+SLOTS = PIECES + LAG_O_OUT + 1
+
+SHARE_PLAIN = 288
+SHARE_HEAD = 152
+HEAD_SLOTS = PASSES + 1
+RAW_TILES = 22
 
 
 def tile_bag_lstm_pa_kernel(tc, x, h_prev, c_prev, is_rnn, W, b, out_0, out_1):
     nc = tc.nc
     with ExitStack() as ctx:
         const = ctx.enter_context(tc.tile_pool(name="const", bufs=1))
-        rawp = ctx.enter_context(tc.tile_pool(name="rawp", bufs=N_RAW))
-        grpp = ctx.enter_context(tc.tile_pool(name="grpp", bufs=4))
-        codep = ctx.enter_context(tc.tile_pool(name="codep", bufs=8))
-        keepp = ctx.enter_context(tc.tile_pool(name="keepp", bufs=2))
-        actp = ctx.enter_context(tc.tile_pool(name="actp", bufs=3))
-        fpp = ctx.enter_context(tc.tile_pool(name="fpp", bufs=2))
-        ostp = ctx.enter_context(tc.tile_pool(name="ostp", bufs=10))
-        mxps = ctx.enter_context(tc.psum_pool(name="mxps", bufs=4))
-        tpps = ctx.enter_context(tc.psum_pool(name="tpps", bufs=4))
+        raw_pool = ctx.enter_context(tc.tile_pool(name="raw_pool", bufs=RAW_TILES))
+        grouped_pool = ctx.enter_context(tc.tile_pool(name="grouped_pool", bufs=4))
+        code_pool = ctx.enter_context(tc.tile_pool(name="code_pool", bufs=8))
+        g_pool = ctx.enter_context(tc.tile_pool(name="g_pool", bufs=2))
+        act_pool = ctx.enter_context(tc.tile_pool(name="act_pool", bufs=3))
+        f_pool = ctx.enter_context(tc.tile_pool(name="f_pool", bufs=2))
+        out_pool = ctx.enter_context(tc.tile_pool(name="out_pool", bufs=10))
+        mx_banks = ctx.enter_context(tc.psum_pool(name="mx_banks", bufs=TILES))
+        turn_banks = ctx.enter_context(tc.psum_pool(name="turn_banks", bufs=ROW_TILES))
         ctx.enter_context(tc.manual_schedule())
 
-        state = {"issued": 0, "released": 0, "act_units": 0, "quantised": 0, "multiplied": 0}
+        count = {"loads": 0, "freed": 0, "quantised": 0, "multiplied": 0, "activated": 0}
 
+        def gate_of(unit):
+            return GATES[unit // 2]
+
+        def due(s, lag, gates=GATES):
+            return [u for u in range(UNITS)
+                    if PASSES * u + PASSES - 1 + lag == s and gate_of(u) in gates]
+
+        zero = const.tile([P, 1], F32, name="zero", tag="zero")
         warm = const.tile([P, 1], F32, name="warm", tag="warm")
-        warm2 = const.tile([P, 1], F32, name="warm2", tag="warm2")
-        nc.vector.memset(warm[:], 0.0)
-        bm_raw = const.tile([P, P], BF16, name="bm_raw", tag="bm_raw")
-        nc.vector.memset(bm_raw[:], 0.0)
-        nc.scalar.dma_start(out=bm_raw[0:32, :], in_=b.rearrange("(r c) -> r c", c=P))
-        nc.scalar.dma_start(out=bm_raw[32:36, :], in_=is_rnn.rearrange("(r p) o -> r (p o)", p=P))
-        nc.scalar.activation(out=warm2[:], in_=warm[:], func=ACT.Sigmoid)
+        nc.vector.memset(zero[:], 0.0)
+        rows_bf = const.tile([P, P], BF16, name="rows_bf", tag="rows_bf")
+        nc.vector.memset(rows_bf[:], 0.0)
+        nc.scalar.dma_start(out=rows_bf[0:32, :], in_=b.rearrange("(r c) -> r c", c=P))
+        nc.scalar.dma_start(out=rows_bf[32:36, :], in_=is_rnn.rearrange("(r p) o -> r (p o)", p=P))
+        nc.scalar.activation(out=warm[:], in_=zero[:], func=ACT.Sigmoid)
         ident = const.tile([P, P], F32, name="ident", tag="ident")
         make_identity(nc, ident[:])
 
-        raws = {}
-        xraws = {}
-        cp_sb = const.tile([P, NBT * H], BF16, name="cp_sb", tag="cp_sb")
+        w_raw = {}
+        x_raw = {}
+        c_sb = const.tile([P, ROW_TILES, H], BF16, name="c_sb", tag="c_sb")
 
         def load_w(n):
-            unit, p = divmod(n, 4)
-            gi, half = divmod(unit, 2)
-            col0 = BLOCK[ROLES[gi]] * H + half * HALF
-            rt = rawp.tile([P, 4 * HALF], BF16, name="raw", tag="raw")
-            raws[n] = rt[:].rearrange("p (t c) -> p t c", t=4)
+            unit, k_pass = divmod(n, PASSES)
+            col = BLOCK[gate_of(unit)] * H + (unit % 2) * UNIT
+            tile_ = raw_pool.tile([P, 4, UNIT], BF16, name="w_raw", tag="raw")
+            w_raw[n] = tile_
             for u in range(2):
-                r0 = 512 * p + 256 * u
+                row = K_PASS * k_pass + 256 * u
                 nc.sync.dma_start(
-                    out=raws[n][:, 2 * u : 2 * u + 2, :],
-                    in_=W[r0 : r0 + 256, col0 : col0 + HALF].rearrange("(q e) c -> q e c", e=2),
+                    out=tile_[:, 2 * u : 2 * u + 2, :],
+                    in_=W[row : row + 256, col : col + UNIT].rearrange("(q e) c -> q e c", e=2),
                 )
 
-        def load_x(p):
-            src = x if p < 2 else h_prev
-            c0 = (p % 2) * 512
-            xt = rawp.tile([P, NBT * 512], BF16, name="xraw", tag="raw")
-            xraws[p] = xt
+        def load_x(k_pass):
+            src = x if k_pass < 2 else h_prev
+            col = (k_pass % 2) * K_PASS
+            tile_ = raw_pool.tile([P, ROW_TILES * K_PASS], BF16, name="x_raw", tag="raw")
+            x_raw[k_pass] = tile_
             nc.sync.dma_start(
-                out=xt[:].rearrange("p (t c) -> p t c", t=NBT),
-                in_=src[:, c0 : c0 + 512].rearrange("(t p) c -> p t c", p=P),
+                out=tile_[:].rearrange("p (r c) -> p r c", r=ROW_TILES),
+                in_=src[:, col : col + K_PASS].rearrange("(r p) c -> p r c", p=P),
             )
 
-        def load_cp():
-            nc.sync.dma_start(
-                out=cp_sb[:].rearrange("p (t c) -> p t c", t=NBT),
-                in_=c_prev.rearrange("(t p) c -> p t c", p=P),
-            )
+        load_order = []
+        for n in range(PIECES):
+            if n == 2 * PASSES * GATES.index("i"):
+                load_order.append(("c", 0))
+            load_order.append(("w", n))
+            if n < PASSES:
+                load_order.append(("x", n))
 
-        loads = []
-        for n in range(NP):
-            loads.append(("w", n))
-            if n < 4:
-                loads.append(("x", n))
-
-        def pump():
-            while state["issued"] < len(loads) and state["issued"] - state["released"] < N_RAW:
-                kind, n = loads[state["issued"]]
-                if kind == "w":
-                    if n == CP_BEFORE:
-                        load_cp()
+        def load_ahead():
+            while count["loads"] < len(load_order) and count["loads"] - count["freed"] < RAW_TILES:
+                what, n = load_order[count["loads"]]
+                if what == "w":
                     load_w(n)
-                else:
+                elif what == "x":
                     load_x(n)
-                state["issued"] += 1
-
-        pump()
-
-        bmT = const.tile([P, 36], F32, name="bmT", tag="bmT")
-        om = const.tile([P, NBT], F32, name="om", tag="om")
-
-        def prep_bias():
-            bm_f = const.tile([P, P], F32, name="bm_f", tag="bm_f")
-            nc.vector.tensor_copy(out=bm_f[:], in_=bm_raw[:])
-            bm_ps = tpps.tile([P, 512], F32, name="bm_ps", tag="tp")
-            nc.tensor.transpose(bm_ps[:, 0:P], bm_f[:], ident[:])
-            nc.vector.tensor_copy(out=bmT[:], in_=bm_ps[:, 0:36])
-            nc.vector.tensor_scalar(
-                out=om[:], in0=bmT[:, 32:36], scalar1=-1.0, scalar2=1.0, op0=ALU.mult, op1=ALU.add
-            )
-
-        def m_col(bt):
-            return bmT[:, 32 + bt : 33 + bt]
-
-        xcodes = const.tile([P, 4 * B], U32, name="xcodes", tag="xcodes", align_bytes=64)
-        xplane = const.tile([P, 4 * B], U8, name="xplane", tag="xplane", align_bytes=64)
-        xgs = {}
-
-        def xcopy(p):
-            s32 = xraws[p][:].bitcast(F32)
-            xg = grpp.tile([P, 4 * B], BF16, name="xg", tag="grp", align_bytes=64)
-            xgs[p] = xg
-            xg32 = xg[:].bitcast(F32).rearrange("p (n u) -> p n u", u=2)
-            for bp in range(2):
-                xt = tpps.tile([P, 512], F32, name="xt", tag="tp")
-                xtv = xt[:].rearrange("p (u n) -> p u n", u=2)
-                for u in range(2):
-                    for b2 in range(2):
-                        w0 = (2 * bp + b2) * 256 + u * P
-                        nc.tensor.transpose(
-                            xtv[:, u, b2 * P : (b2 + 1) * P], s32[:, w0 : w0 + P], ident[:]
-                        )
-                dst = xg32[:, bp * 256 : (bp + 1) * 256, :]
-                srcv = xt[:].rearrange("p (u n) -> p n u", u=2)
-                if bp == 0:
-                    nc.vector.tensor_copy(out=dst, in_=srcv)
                 else:
-                    nc.scalar.copy(out=dst, in_=srcv)
-            state["released"] += 1
-            pump()
+                    nc.sync.dma_start(out=c_sb[:], in_=c_prev.rearrange("(r p) c -> p r c", p=P))
+                    count["freed"] += 1
+                count["loads"] += 1
 
-        def xquant(p):
-            nc.vector.quantize_mx(
-                out=xcodes[:, p * B : (p + 1) * B].bitcast(FP8X4),
-                scales=xplane[:, p * B : (p + 1) * B],
-                in_=xgs[p][:],
-            )
+        load_ahead()
 
-        grps = {}
-        codes = {}
+        cols = const.tile([P, 36], F32, name="cols", tag="cols")
+        one_minus_m = const.tile([P, ROW_TILES], F32, name="one_minus_m", tag="one_minus_m")
+
+        def turn_bias_and_m():
+            rows_f32 = const.tile([P, P], F32, name="rows_f32", tag="rows_f32")
+            nc.vector.tensor_copy(out=rows_f32[:], in_=rows_bf[:])
+            bank = turn_banks.tile([P, 512], F32, name="bank", tag="turn")
+            nc.tensor.transpose(bank[:, 0:P], rows_f32[:], ident[:])
+            nc.vector.tensor_copy(out=cols[:], in_=bank[:, 0:36])
+            nc.vector.tensor_scalar(out=one_minus_m[:], in0=cols[:, 32:36], scalar1=-1.0, scalar2=1.0,
+                                    op0=ALU.mult, op1=ALU.add)
+
+        def m_of(r):
+            return cols[:, 32 + r : 33 + r]
+
+        x_codes = const.tile([P, PASSES, B], U32, name="x_codes", tag="x_codes", align_bytes=64)
+        x_scales = const.tile([P, PASSES, B], U8, name="x_scales", tag="x_scales", align_bytes=64)
+        x_grouped = {}
+
+        def turn_x(k_pass):
+            words = x_raw[k_pass][:].bitcast(F32)
+            grouped = grouped_pool.tile([P, 4 * B], BF16, name="x_grouped", tag="grouped", align_bytes=64)
+            x_grouped[k_pass] = grouped
+            pairs = grouped[:].bitcast(F32).rearrange("p (n u) -> p n u", u=2)
+            for half in range(2):
+                bank = turn_banks.tile([P, 512], F32, name="bank", tag="turn")
+                by_u = bank[:].rearrange("p (u n) -> p u n", u=2)
+                for u in range(2):
+                    for r in range(2):
+                        word = (2 * half + r) * 256 + u * P
+                        nc.tensor.transpose(by_u[:, u, r * P : (r + 1) * P], words[:, word : word + P], ident[:])
+                dst = pairs[:, half * 256 : (half + 1) * 256, :]
+                src = bank[:].rearrange("p (u n) -> p n u", u=2)
+                if half == 0:
+                    nc.vector.tensor_copy(out=dst, in_=src)
+                else:
+                    nc.scalar.copy(out=dst, in_=src)
+            count["freed"] += 1
+            load_ahead()
+
+        def quantise_x(k_pass):
+            nc.vector.quantize_mx(out=x_codes[:, k_pass, :].bitcast(FP8X4), scales=x_scales[:, k_pass, :],
+                                  in_=x_grouped[k_pass][:])
+
+        w_grouped = {}
+        w_codes = {}
         banks = {}
-        keep = {}
-        acts = {}
-        fps = {}
-        tbs = {}
+
+        def vector_share(s):
+            if s < HEAD_SLOTS:
+                return SHARE_HEAD
+            scalar_busy = due(s, LAG_ACTIVATE) or due(s, LAG_F_BLEND, "f") or due(s, LAG_O_OUT, "o")
+            vector_busy = due(s, LAG_F_TIMES_C, "f") or due(s, LAG_I_TIMES_G, "i") or due(s, LAG_C_OUT, "i")
+            if scalar_busy and not vector_busy:
+                return UNIT
+            if vector_busy and not scalar_busy:
+                return 0
+            return SHARE_PLAIN
 
         def regroup(n):
-            rv = raws[n]
-            grp = grpp.tile([P, 4 * HALF], BF16, name="grp", tag="grp", align_bytes=64)
-            grps[n] = grp
-            gv = grp[:].rearrange("p (c t) -> p c t", t=4)
-            a = SHARES[n]
-            if a > 0:
+            grouped = grouped_pool.tile([P, UNIT, 4], BF16, name="w_grouped", tag="grouped", align_bytes=64)
+            w_grouped[n] = grouped
+            split = vector_share(n)
+            if split > 0:
                 nc.vector.tensor_copy(
-                    out=gv[:, 0:a, :].rearrange("p (c i) t -> p c t i", i=4),
-                    in_=rv[:, :, 0:a].rearrange("p t (c i) -> p c t i", i=4),
+                    out=grouped[:, 0:split, :].rearrange("p (c i) t -> p c t i", i=4),
+                    in_=w_raw[n][:, :, 0:split].rearrange("p t (c i) -> p c t i", i=4),
                 )
-            if a < HALF:
+            if split < UNIT:
                 nc.scalar.copy(
-                    out=gv[:, a:HALF, :].rearrange("p (c i) t -> p c t i", i=4),
-                    in_=rv[:, :, a:HALF].rearrange("p t (c i) -> p c t i", i=4),
+                    out=grouped[:, split:UNIT, :].rearrange("p (c i) t -> p c t i", i=4),
+                    in_=w_raw[n][:, :, split:UNIT].rearrange("p t (c i) -> p c t i", i=4),
                 )
-            state["released"] += 1
-            pump()
+            count["freed"] += 1
+            load_ahead()
 
         def quantise(n):
-            wc = codep.tile([P, HALF], U32, name="wc", tag="wc", align_bytes=64)
-            wp = codep.tile([P, HALF], U8, name="wp", tag="wp", align_bytes=64)
-            nc.vector.quantize_mx(out=wc[:].bitcast(FP8X4), scales=wp[:], in_=grps[n][:])
-            codes[n] = (wc, wp)
-            state["quantised"] += 1
+            codes = code_pool.tile([P, UNIT], U32, name="codes", tag="codes", align_bytes=64)
+            scales = code_pool.tile([P, UNIT], U8, name="scales", tag="scales", align_bytes=64)
+            nc.vector.quantize_mx(out=codes[:].bitcast(FP8X4), scales=scales[:],
+                                  in_=w_grouped[n][:].rearrange("p c t -> p (c t)"))
+            w_codes[n] = (codes, scales)
+            count["quantised"] += 1
 
-        def matmuls(n):
-            unit, p = divmod(n, 4)
-            wc, wp = codes[n]
-            for jj in range(4):
-                if p == 0:
-                    bank = mxps.tile([P, B], F32, name="bank", tag="mx")
-                    banks[(unit, jj)] = bank
+        def multiply(n):
+            unit, k_pass = divmod(n, PASSES)
+            codes, scales = w_codes[n]
+            for j in range(TILES):
+                if k_pass == 0:
+                    bank = mx_banks.tile([P, B], F32, name="bank", tag="mx")
+                    banks[(unit, j)] = bank
                 nc.tensor.matmul_mx(
-                    out=banks[(unit, jj)][:],
-                    lhsT=wc[:, jj * P : (jj + 1) * P].bitcast(FP8X4),
-                    lhsT_scale=wp[:, jj * P : (jj + 1) * P],
-                    rhs=xcodes[:, p * B : (p + 1) * B].bitcast(FP8X4),
-                    rhs_scale=xplane[:, p * B : (p + 1) * B],
-                    start=(p == 0),
-                    stop=(p == 3),
+                    out=banks[(unit, j)][:],
+                    lhsT=codes[:, j * P : (j + 1) * P].bitcast(FP8X4),
+                    lhsT_scale=scales[:, j * P : (j + 1) * P],
+                    rhs=x_codes[:, k_pass, :].bitcast(FP8X4),
+                    rhs_scale=x_scales[:, k_pass, :],
+                    start=(k_pass == 0),
+                    stop=(k_pass == PASSES - 1),
                 )
 
-        def flush():
-            while state["multiplied"] < state["quantised"] and (
-                state["multiplied"] % 4 != 0 or state["act_units"] >= state["multiplied"] // 4
+        def multiply_what_is_ready():
+            while count["multiplied"] < count["quantised"] and (
+                count["multiplied"] % PASSES != 0 or count["activated"] >= count["multiplied"] // PASSES
             ):
-                matmuls(state["multiplied"])
-                state["multiplied"] += 1
+                multiply(count["multiplied"])
+                count["multiplied"] += 1
 
-        def activations(unit):
-            gi, half = divmod(unit, 2)
-            role = ROLES[gi]
-            if role == "g":
-                aT = keepp.tile([P, 4, B], F32, name="gT", tag="gT")
-                keep[half] = aT
+        acts = {}
+        turned = {}
+        f_part = {}
+
+        def activate(unit):
+            gate = gate_of(unit)
+            pool = g_pool if gate == "g" else act_pool
+            act = pool.tile([P, TILES, B], F32, name="act", tag="act")
+            acts[unit] = act
+            for j in range(TILES):
+                col = BLOCK[gate] * (H // P) + (unit % 2) * TILES + j
+                nc.scalar.activation(out=act[:, j, :], in_=banks[(unit, j)][:],
+                                     func=ACT.Tanh if gate == "g" else ACT.Sigmoid,
+                                     bias=cols[:, col : col + 1], scale=1.0)
+            count["activated"] += 1
+
+        def turn_back(unit, src):
+            for r in range(ROW_TILES):
+                bank = turn_banks.tile([P, UNIT], F32, name="bank", tag="turn")
+                turned[(unit, r)] = bank
+                for j in range(TILES):
+                    nc.tensor.transpose(bank[:, j * P : (j + 1) * P], src[:, j, r * P : (r + 1) * P], ident[:])
+
+        def blend(engine, dst, unit, r):
+            if engine == "scalar":
+                nc.scalar.activation(out=dst, in_=turned[(unit, r)][:], func=ACT.Identity,
+                                     bias=one_minus_m[:, r : r + 1], scale=m_of(r))
             else:
-                aT = actp.tile([P, 4, B], F32, name="aT", tag="aT")
-            acts[unit] = aT
-            for jj in range(4):
-                col = BLOCK[role] * 8 + half * 4 + jj
-                nc.scalar.activation(
-                    out=aT[:, jj, :],
-                    in_=banks[(unit, jj)][:],
-                    func=ACT.Tanh if role == "g" else ACT.Sigmoid,
-                    bias=bmT[:, col : col + 1],
-                    scale=1.0,
-                )
-            state["act_units"] += 1
+                nc.vector.tensor_scalar(out=dst, in0=turned[(unit, r)][:], scalar1=m_of(r),
+                                        scalar2=one_minus_m[:, r : r + 1], op0=ALU.mult, op1=ALU.add)
 
-        def transposes(key, srcT, pool, tag):
-            for bt in range(NBT):
-                tb = pool.tile([P, 512], F32, name="tb", tag=tag)
-                tbs[(key, bt)] = tb
-                for jj in range(4):
-                    nc.tensor.transpose(
-                        tb[:, jj * P : (jj + 1) * P], srcT[:, jj, bt * P : (bt + 1) * P], ident[:]
-                    )
+        def f_blend(unit):
+            part = f_pool.tile([P, ROW_TILES, UNIT], F32, name="part", tag="part")
+            f_part[unit % 2] = part
+            for r in range(ROW_TILES):
+                blend("scalar", part[:, r, :], unit, r)
 
-        def blend_scalar(dst, tb, bt):
-            nc.scalar.activation(
-                out=dst, in_=tb[:], func=ACT.Identity, bias=om[:, bt : bt + 1], scale=m_col(bt)
-            )
+        def f_times_c(unit):
+            half = unit % 2
+            nc.vector.tensor_tensor(out=f_part[half][:], in0=f_part[half][:],
+                                    in1=c_sb[:, :, half * UNIT : (half + 1) * UNIT], op=ALU.mult)
 
-        def blend_vector(dst, tb, bt):
-            nc.vector.tensor_scalar(
-                out=dst, in0=tb[:], scalar1=m_col(bt), scalar2=om[:, bt : bt + 1],
-                op0=ALU.mult, op1=ALU.add,
-            )
+        def i_times_g(unit):
+            g_act = acts[GATES.index("g") * 2 + unit % 2]
+            nc.vector.tensor_tensor(out=g_act[:], in0=acts[unit][:], in1=g_act[:], op=ALU.mult)
 
-        def mul_ig(half, unit):
-            nc.vector.tensor_tensor(out=keep[half][:], in0=acts[unit][:], in1=keep[half][:], op=ALU.mult)
+        def c_out(unit):
+            half = unit % 2
+            turn_back(unit, acts[GATES.index("g") * 2 + half])
+            for r in range(ROW_TILES):
+                res = out_pool.tile([P, UNIT], F32, name="res", tag="res")
+                nc.vector.scalar_tensor_tensor(out=res[:], in0=turned[(unit, r)][:], scalar=m_of(r),
+                                               in1=f_part[half][:, r, :], op0=ALU.mult, op1=ALU.add)
+                nc.sync.dma_start(out=out_0[r * P : (r + 1) * P, half * UNIT : (half + 1) * UNIT], in_=res[:])
 
-        def f_blend(half):
-            fp = fpp.tile([P, NBT, HALF], F32, name="fp", tag="fp")
-            fps[half] = fp
-            for bt in range(NBT):
-                blend_scalar(fp[:, bt, :], tbs[(("f", half), bt)], bt)
+        def o_out(unit):
+            half = unit % 2
+            for r in range(ROW_TILES):
+                res = out_pool.tile([P, UNIT], F32, name="res", tag="res")
+                blend("vector" if unit == UNITS - 1 and r < 2 else "scalar", res[:], unit, r)
+                nc.sync.dma_start(out=out_1[r * P : (r + 1) * P, half * UNIT : (half + 1) * UNIT], in_=res[:])
 
-        def f_times_c(half):
-            cols = slice(half * HALF, (half + 1) * HALF)
-            cpv = cp_sb[:].rearrange("p (t c) -> p t c", t=NBT)[:, :, cols]
-            nc.vector.tensor_tensor(out=fps[half][:], in0=fps[half][:], in1=cpv, op=ALU.mult)
-
-        def c_out(half):
-            cols = slice(half * HALF, (half + 1) * HALF)
-            for bt in range(NBT):
-                cst = ostp.tile([P, HALF], F32, name="cst", tag="ost")
-                nc.vector.scalar_tensor_tensor(
-                    out=cst[:], in0=tbs[(("ig", half), bt)][:], scalar=m_col(bt),
-                    in1=fps[half][:, bt, :], op0=ALU.mult, op1=ALU.add,
-                )
-                nc.sync.dma_start(out=out_0[bt * P : (bt + 1) * P, cols], in_=cst[:])
-
-        def o_out(half, vector_bts):
-            cols = slice(half * HALF, (half + 1) * HALF)
-            for bt in range(NBT):
-                ost = ostp.tile([P, HALF], F32, name="ost", tag="ost")
-                if bt in vector_bts:
-                    blend_vector(ost[:], tbs[(("o", half), bt)], bt)
-                else:
-                    blend_scalar(ost[:], tbs[(("o", half), bt)], bt)
-                nc.sync.dma_start(out=out_1[bt * P : (bt + 1) * P, cols], in_=ost[:])
-
-        tasks = {}
-
-        def at(name, slot, fn):
-            slot = SLOTS.get(name, slot)
-            tasks[slot] = tasks.get(slot, []) + [fn]
-            return slot
-
-        u_slot = {}
-        for unit in range(8):
-            gi, half = divmod(unit, 2)
-            role = ROLES[gi]
-            s_a = at("A%d" % unit, 4 * unit + 3 + LAG_A, lambda unit=unit: activations(unit))
-            if role == "f":
-                at("Tf%d" % half, s_a + 1,
-                   lambda unit=unit, half=half: transposes(("f", half), acts[unit], tpps, "tp"))
-                s_b = at("fb%d" % half, s_a + 2, lambda half=half: f_blend(half))
-                u_slot[half] = at("u%d" % half, s_b + 1, lambda half=half: f_times_c(half))
-            elif role == "o":
-                if unit == 7:
-                    at("To%d" % half, s_a + 1,
-                       lambda unit=unit, half=half: transposes(("o", half), acts[unit], mxps, "mx"))
-                    at("o%d" % half, s_a + 2, lambda half=half: o_out(half, (0, 1)))
-                else:
-                    at("To%d" % half, s_a + 1,
-                       lambda unit=unit, half=half: transposes(("o", half), acts[unit], tpps, "tp"))
-                    at("o%d" % half, s_a + 2, lambda half=half: o_out(half, ()))
-            elif role == "i":
-                s_i = at("ig%d" % half, s_a + 1, lambda unit=unit, half=half: mul_ig(half, unit))
-                s_t = at("Tig%d" % half, max(s_i + 1, u_slot[half]),
-                         lambda half=half: transposes(("ig", half), keep[half], tpps, "tp"))
-                at("c%d" % half, s_t + 1, lambda half=half: c_out(half))
-
-        for s in range(NP + 6):
-            if s < NP:
+        for s in range(SLOTS):
+            if s < PIECES:
                 regroup(s)
-            if 1 <= s <= NP:
+            if 1 <= s <= PIECES:
                 quantise(s - 1)
-            if 1 <= s <= 4:
-                xquant(s - 1)
-            if s < 4:
-                xcopy(s)
-            if s == BIAS_SLOT:
-                prep_bias()
-            if s in MM_FIRST:
-                flush()
-            for fn in tasks.get(s, []):
-                fn()
-            flush()
+            if 1 <= s <= PASSES:
+                quantise_x(s - 1)
+            if s < PASSES:
+                turn_x(s)
+            if s == PASSES:
+                turn_bias_and_m()
+            for unit in due(s, LAG_F_BLEND, "f"):
+                f_blend(unit)
+            for unit in due(s, LAG_F_TIMES_C, "f"):
+                f_times_c(unit)
+            for unit in due(s, LAG_I_TIMES_G, "i"):
+                i_times_g(unit)
+            for unit in due(s, LAG_C_OUT, "i"):
+                c_out(unit)
+            for unit in due(s, LAG_O_OUT, "o"):
+                o_out(unit)
+            for unit in due(s, LAG_ACTIVATE):
+                activate(unit)
+            for unit in due(s, LAG_TRANSPOSE, "fo"):
+                turn_back(unit, acts[unit])
+            multiply_what_is_ready()

@@ -86,12 +86,11 @@ def tile_bag_lstm_pa_kernel(tc, x, h_prev, c_prev, is_rnn, W, b, out_0, out_1):
             col = BLOCK[gate_of(unit)] * H + (unit % 2) * UNIT
             tile_ = raw_pool.tile([P, 4, UNIT], BF16, name="w_raw", tag="raw")
             w_raw[n] = tile_
-            for u in range(2):
-                row = K_PASS * k_pass + 256 * u
-                nc.sync.dma_start(
-                    out=tile_[:, 2 * u : 2 * u + 2, :],
-                    in_=W[row : row + 256, col : col + UNIT].rearrange("(q e) c -> q e c", e=2),
-                )
+            row = K_PASS * k_pass
+            nc.sync.dma_start(
+                out=tile_[:],
+                in_=W[row : row + K_PASS, col : col + UNIT].rearrange("(q t) c -> q t c", t=4),
+            )
 
         def load_x(k_pass):
             src = x if k_pass < 2 else h_prev
@@ -145,7 +144,7 @@ def tile_bag_lstm_pa_kernel(tc, x, h_prev, c_prev, is_rnn, W, b, out_0, out_1):
         x_grouped = {}
 
         def turn_x(k_pass):
-            words = x_raw[k_pass][:].bitcast(F32)
+            words = x_raw[k_pass][:].bitcast(F32).rearrange("p (r q u) -> p r u q", r=ROW_TILES, u=2)
             grouped = grouped_pool.tile([P, 4 * B], BF16, name="x_grouped", tag="grouped", align_bytes=64)
             x_grouped[k_pass] = grouped
             pairs = grouped[:].bitcast(F32).rearrange("p (n u) -> p n u", u=2)
@@ -154,8 +153,7 @@ def tile_bag_lstm_pa_kernel(tc, x, h_prev, c_prev, is_rnn, W, b, out_0, out_1):
                 by_u = bank[:].rearrange("p (u n) -> p u n", u=2)
                 for u in range(2):
                     for r in range(2):
-                        word = (2 * half + r) * 256 + u * P
-                        nc.tensor.transpose(by_u[:, u, r * P : (r + 1) * P], words[:, word : word + P], ident[:])
+                        nc.tensor.transpose(by_u[:, u, r * P : (r + 1) * P], words[:, 2 * half + r, u, :], ident[:])
                 dst = pairs[:, half * 256 : (half + 1) * 256, :]
                 src = bank[:].rearrange("p (u n) -> p n u", u=2)
                 if half == 0:

@@ -36,7 +36,7 @@ LAG_C_OUT = 10
 LAG_O_OUT = 5
 SLOTS = PIECES + LAG_O_OUT + 1
 
-SHARE_PLAIN = 288
+SHARE_PLAIN = 256
 SHARE_HEAD = 152
 HEAD_SLOTS = PASSES + 1
 RAW_TILES = 22

@@ -30,16 +30,17 @@ PIECES = UNITS * PASSES
 LAG_ACTIVATE = 3
 LAG_TRANSPOSE = 4
 LAG_F_BLEND = 6
-LAG_F_TIMES_C = 7
-LAG_I_TIMES_G = 9
-LAG_C_OUT = 10
+LAG_F_TIMES_C = 8
+LAG_I_TIMES_G = 10
+LAG_C_OUT = 11
 LAG_O_OUT = 5
 SLOTS = PIECES + LAG_O_OUT + 1
 
-SHARE_PLAIN = 256
+SHARE_PLAIN = 288
 SHARE_HEAD = 152
 HEAD_SLOTS = PASSES + 1
 RAW_TILES = 22
+C_PREV_BEFORE_PIECE = 18
 
 
 def tile_bag_lstm_pa_kernel(tc, x, h_prev, c_prev, is_rnn, W, b, out_0, out_1):
@@ -104,7 +105,7 @@ def tile_bag_lstm_pa_kernel(tc, x, h_prev, c_prev, is_rnn, W, b, out_0, out_1):
 
         load_order = []
         for n in range(PIECES):
-            if n == 2 * PASSES * GATES.index("i"):
+            if n == C_PREV_BEFORE_PIECE:
                 load_order.append(("c", 0))
             load_order.append(("w", n))
             if n < PASSES:

@@ -40,7 +40,6 @@ SHARE_PLAIN = 288
 SHARE_HEAD = 152
 HEAD_SLOTS = PASSES + 1
 RAW_TILES = 22
-C_PREV_BEFORE_PIECE = 18
 
 
 def tile_bag_lstm_pa_kernel(tc, x, h_prev, c_prev, is_rnn, W, b, out_0, out_1):
@@ -80,7 +79,7 @@ def tile_bag_lstm_pa_kernel(tc, x, h_prev, c_prev, is_rnn, W, b, out_0, out_1):
 
         w_raw = {}
         x_raw = {}
-        c_sb = const.tile([P, ROW_TILES, H], BF16, name="c_sb", tag="c_sb")
+        c_sb = const.tile([P, 2, ROW_TILES, UNIT], BF16, name="c_sb", tag="c_sb")
 
         def load_w(n):
             unit, k_pass = divmod(n, PASSES)
@@ -103,10 +102,16 @@ def tile_bag_lstm_pa_kernel(tc, x, h_prev, c_prev, is_rnn, W, b, out_0, out_1):
                 in_=src[:, col : col + K_PASS].rearrange("(r p) c -> p r c", p=P),
             )
 
+        def load_c(half):
+            nc.sync.dma_start(
+                out=c_sb[:, half, :, :],
+                in_=c_prev[:, half * UNIT : (half + 1) * UNIT].rearrange("(r p) c -> p r c", p=P),
+            )
+
         load_order = []
         for n in range(PIECES):
-            if n == C_PREV_BEFORE_PIECE:
-                load_order.append(("c", 0))
+            for unit in due(n + 1, LAG_F_TIMES_C, "f"):
+                load_order.append(("c", unit % 2))
             load_order.append(("w", n))
             if n < PASSES:
                 load_order.append(("x", n))
@@ -119,7 +124,7 @@ def tile_bag_lstm_pa_kernel(tc, x, h_prev, c_prev, is_rnn, W, b, out_0, out_1):
                 elif what == "x":
                     load_x(n)
                 else:
-                    nc.sync.dma_start(out=c_sb[:], in_=c_prev.rearrange("(r p) c -> p r c", p=P))
+                    load_c(n)
                     count["freed"] += 1
                 count["loads"] += 1
 
@@ -255,24 +260,20 @@ def tile_bag_lstm_pa_kernel(tc, x, h_prev, c_prev, is_rnn, W, b, out_0, out_1):
                 for j in range(TILES):
                     nc.tensor.transpose(bank[:, j * P : (j + 1) * P], src[:, j, r * P : (r + 1) * P], ident[:])
 
-        def blend(engine, dst, unit, r):
-            if engine == "scalar":
-                nc.scalar.activation(out=dst, in_=turned[(unit, r)][:], func=ACT.Identity,
-                                     bias=one_minus_m[:, r : r + 1], scale=m_of(r))
-            else:
-                nc.vector.tensor_scalar(out=dst, in0=turned[(unit, r)][:], scalar1=m_of(r),
-                                        scalar2=one_minus_m[:, r : r + 1], op0=ALU.mult, op1=ALU.add)
+        def blend(dst, unit, r):
+            nc.scalar.activation(out=dst, in_=turned[(unit, r)][:], func=ACT.Identity,
+                                 bias=one_minus_m[:, r : r + 1], scale=m_of(r))
 
         def f_blend(unit):
             part = f_pool.tile([P, ROW_TILES, UNIT], F32, name="part", tag="part")
             f_part[unit % 2] = part
             for r in range(ROW_TILES):
-                blend("scalar", part[:, r, :], unit, r)
+                blend(part[:, r, :], unit, r)
 
         def f_times_c(unit):
             half = unit % 2
             nc.vector.tensor_tensor(out=f_part[half][:], in0=f_part[half][:],
-                                    in1=c_sb[:, :, half * UNIT : (half + 1) * UNIT], op=ALU.mult)
+                                    in1=c_sb[:, half, :, :], op=ALU.mult)
 
         def i_times_g(unit):
             g_act = acts[GATES.index("g") * 2 + unit % 2]
@@ -291,7 +292,7 @@ def tile_bag_lstm_pa_kernel(tc, x, h_prev, c_prev, is_rnn, W, b, out_0, out_1):
             half = unit % 2
             for r in range(ROW_TILES):
                 res = out_pool.tile([P, UNIT], F32, name="res", tag="res")
-                blend("vector" if unit == UNITS - 1 and r < 2 else "scalar", res[:], unit, r)
+                blend(res[:], unit, r)
                 nc.sync.dma_start(out=out_1[r * P : (r + 1) * P, half * UNIT : (half + 1) * UNIT], in_=res[:])
 
         for s in range(SLOTS):

@@ -145,13 +145,13 @@ def tile_bag_lstm_pa_kernel(tc, x, h_prev, c_prev, is_rnn, W, b, out_0, out_1):
         def m_of(r):
             return cols[:, 32 + r : 33 + r]
 
-        x_codes = const.tile([P, PASSES, B], U32, name="x_codes", tag="x_codes", align_bytes=64)
-        x_scales = const.tile([P, PASSES, B], U8, name="x_scales", tag="x_scales", align_bytes=64)
+        x_codes = const.tile([P, PASSES, B], U32, name="x_codes", tag="x_codes", align_bytes=256)
+        x_scales = const.tile([P, PASSES, B], U8, name="x_scales", tag="x_scales", align_bytes=256)
         x_grouped = {}
 
         def turn_x(k_pass):
             words = x_raw[k_pass][:].bitcast(F32).rearrange("p (r q u) -> p r u q", r=ROW_TILES, u=2)
-            grouped = grouped_pool.tile([P, 4 * B], BF16, name="x_grouped", tag="grouped", align_bytes=64)
+            grouped = grouped_pool.tile([P, 4 * B], BF16, name="x_grouped", tag="grouped", align_bytes=256)
             x_grouped[k_pass] = grouped
             pairs = grouped[:].bitcast(F32).rearrange("p (n u) -> p n u", u=2)
             for half in range(2):
@@ -189,7 +189,7 @@ def tile_bag_lstm_pa_kernel(tc, x, h_prev, c_prev, is_rnn, W, b, out_0, out_1):
             return SHARE_PLAIN
 
         def regroup(n):
-            grouped = grouped_pool.tile([P, UNIT, 4], BF16, name="w_grouped", tag="grouped", align_bytes=64)
+            grouped = grouped_pool.tile([P, UNIT, 4], BF16, name="w_grouped", tag="grouped", align_bytes=256)
             w_grouped[n] = grouped
             split = vector_share(n)
             if split > 0:
@@ -206,8 +206,8 @@ def tile_bag_lstm_pa_kernel(tc, x, h_prev, c_prev, is_rnn, W, b, out_0, out_1):
             load_ahead()
 
         def quantise(n):
-            codes = code_pool.tile([P, UNIT], U32, name="codes", tag="codes", align_bytes=64)
-            scales = code_pool.tile([P, UNIT], U8, name="scales", tag="scales", align_bytes=64)
+            codes = code_pool.tile([P, UNIT], U32, name="codes", tag="codes", align_bytes=256)
+            scales = code_pool.tile([P, UNIT], U8, name="scales", tag="scales", align_bytes=256)
             nc.vector.quantize_mx(out=codes[:].bitcast(FP8X4), scales=scales[:],
                                   in_=w_grouped[n][:].rearrange("p c t -> p (c t)"))
             w_codes[n] = (codes, scales)

@@ -39,6 +39,7 @@ SLOTS = PIECES + LAG_O_OUT + 1
 SHARE_PLAIN = 288
 SHARE_HEAD = 152
 HEAD_SLOTS = PASSES + 1
+X_CHUNKS = {0: (0, 1), 1: (2, 3)}
 RAW_TILES = 22
 
 
@@ -57,7 +58,7 @@ def tile_bag_lstm_pa_kernel(tc, x, h_prev, c_prev, is_rnn, W, b, out_0, out_1):
         turn_banks = ctx.enter_context(tc.psum_pool(name="turn_banks", bufs=ROW_TILES))
         ctx.enter_context(tc.manual_schedule())
 
-        count = {"loads": 0, "freed": 0, "quantised": 0, "multiplied": 0, "activated": 0}
+        count = {"loads": 0, "freed": 0, "quantised": 0, "multiplied": 0, "activated": 0, "x": 0}
 
         def gate_of(unit):
             return GATES[unit // 2]
@@ -72,14 +73,15 @@ def tile_bag_lstm_pa_kernel(tc, x, h_prev, c_prev, is_rnn, W, b, out_0, out_1):
         rows_bf = const.tile([P, P], BF16, name="rows_bf", tag="rows_bf")
         nc.vector.memset(rows_bf[:], 0.0)
         nc.scalar.dma_start(out=rows_bf[0:32, :], in_=b.rearrange("(r c) -> r c", c=P))
-        nc.scalar.dma_start(out=rows_bf[32:36, :], in_=is_rnn.rearrange("(r p) o -> r (p o)", p=P))
+        m_bf = const.tile([P, ROW_TILES], BF16, name="m_bf", tag="m_bf")
+        nc.scalar.dma_start(out=m_bf[:], in_=is_rnn.rearrange("(p r) o -> p (r o)", r=ROW_TILES))
         nc.scalar.activation(out=warm[:], in_=zero[:], func=ACT.Sigmoid)
         ident = const.tile([P, P], F32, name="ident", tag="ident")
         make_identity(nc, ident[:])
 
         w_raw = {}
         x_raw = {}
-        c_sb = const.tile([P, 2, ROW_TILES, UNIT], BF16, name="c_sb", tag="c_sb")
+        c_sb = const.tile([P, ROW_TILES, H], BF16, name="c_sb", tag="c_sb")
 
         def load_w(n):
             unit, k_pass = divmod(n, PASSES)
@@ -92,29 +94,24 @@ def tile_bag_lstm_pa_kernel(tc, x, h_prev, c_prev, is_rnn, W, b, out_0, out_1):
                 in_=W[row : row + K_PASS, col : col + UNIT].rearrange("(q t) c -> q t c", t=4),
             )
 
-        def load_x(k_pass):
-            src = x if k_pass < 2 else h_prev
-            col = (k_pass % 2) * K_PASS
-            tile_ = raw_pool.tile([P, ROW_TILES * K_PASS], BF16, name="x_raw", tag="raw")
-            x_raw[k_pass] = tile_
-            nc.sync.dma_start(
-                out=tile_[:].rearrange("p (r c) -> p r c", r=ROW_TILES),
-                in_=src[:, col : col + K_PASS].rearrange("(r p) c -> p r c", p=P),
-            )
+        def load_x(n):
+            src = (x if n < 2 else h_prev).rearrange("(p r) c -> p r c", r=ROW_TILES)
+            tile_ = raw_pool.tile([P, 2, H], BF16, name="x_raw", tag="raw")
+            x_raw[n] = tile_
+            nc.sync.dma_start(out=tile_[:], in_=src[:, 2 * (n % 2) : 2 * (n % 2) + 2, :])
 
-        def load_c(half):
+        def load_c():
             nc.sync.dma_start(
-                out=c_sb[:, half, :, :],
-                in_=c_prev[:, half * UNIT : (half + 1) * UNIT].rearrange("(r p) c -> p r c", p=P),
+                out=c_sb[:], in_=c_prev.rearrange("(p r) c -> p r c", r=ROW_TILES),
             )
 
         load_order = []
         for n in range(PIECES):
-            for unit in due(n + 1, LAG_F_TIMES_C, "f"):
-                load_order.append(("c", unit % 2))
+            if due(n + 1, LAG_F_TIMES_C, "f") and ("c",0) not in load_order:
+                load_order.append(("c", 0))
             load_order.append(("w", n))
-            if n < PASSES:
-                load_order.append(("x", n))
+            for chunk in X_CHUNKS.get(n, ()):
+                load_order.append(("x", chunk))
 
         def load_ahead():
             while count["loads"] < len(load_order) and count["loads"] - count["freed"] < RAW_TILES:
@@ -124,13 +121,14 @@ def tile_bag_lstm_pa_kernel(tc, x, h_prev, c_prev, is_rnn, W, b, out_0, out_1):
                 elif what == "x":
                     load_x(n)
                 else:
-                    load_c(n)
+                    load_c()
                     count["freed"] += 1
                 count["loads"] += 1
 
         load_ahead()
 
-        cols = const.tile([P, 36], F32, name="cols", tag="cols")
+        cols = const.tile([P, 32], F32, name="cols", tag="cols")
+        m_cols = const.tile([P, ROW_TILES], F32, name="m_cols", tag="m_cols")
         one_minus_m = const.tile([P, ROW_TILES], F32, name="one_minus_m", tag="one_minus_m")
 
         def turn_bias_and_m():
@@ -138,40 +136,44 @@ def tile_bag_lstm_pa_kernel(tc, x, h_prev, c_prev, is_rnn, W, b, out_0, out_1):
             nc.vector.tensor_copy(out=rows_f32[:], in_=rows_bf[:])
             bank = turn_banks.tile([P, 512], F32, name="bank", tag="turn")
             nc.tensor.transpose(bank[:, 0:P], rows_f32[:], ident[:])
-            nc.vector.tensor_copy(out=cols[:], in_=bank[:, 0:36])
-            nc.vector.tensor_scalar(out=one_minus_m[:], in0=cols[:, 32:36], scalar1=-1.0, scalar2=1.0,
+            nc.vector.tensor_copy(out=cols[:], in_=bank[:, 0:32])
+            nc.vector.tensor_copy(out=m_cols[:], in_=m_bf[:])
+            nc.vector.tensor_scalar(out=one_minus_m[:], in0=m_cols[:], scalar1=-1.0, scalar2=1.0,
                                     op0=ALU.mult, op1=ALU.add)
 
         def m_of(r):
-            return cols[:, 32 + r : 33 + r]
+            return m_cols[:, r : r + 1]
 
         x_codes = const.tile([P, PASSES, B], U32, name="x_codes", tag="x_codes", align_bytes=256)
         x_scales = const.tile([P, PASSES, B], U8, name="x_scales", tag="x_scales", align_bytes=256)
         x_grouped = {}
 
-        def turn_x(k_pass):
-            words = x_raw[k_pass][:].bitcast(F32).rearrange("p (r q u) -> p r u q", r=ROW_TILES, u=2)
+        def turn_x(n):
+            words = x_raw[n][:].rearrange("p r c -> p (r c)").bitcast(F32).rearrange("p (r a q u) -> p a r u q", r=2, a=2, u=2)
             grouped = grouped_pool.tile([P, 4 * B], BF16, name="x_grouped", tag="grouped", align_bytes=256)
-            x_grouped[k_pass] = grouped
-            pairs = grouped[:].bitcast(F32).rearrange("p (n u) -> p n u", u=2)
-            for half in range(2):
+            x_grouped[n] = grouped
+            pairs = grouped[:].bitcast(F32).rearrange("p (a n u) -> p a n u", a=2, u=2)
+            for a in range(2):
                 bank = turn_banks.tile([P, 512], F32, name="bank", tag="turn")
                 by_u = bank[:].rearrange("p (u n) -> p u n", u=2)
                 for u in range(2):
                     for r in range(2):
-                        nc.tensor.transpose(by_u[:, u, r * P : (r + 1) * P], words[:, 2 * half + r, u, :], ident[:])
-                dst = pairs[:, half * 256 : (half + 1) * 256, :]
+                        nc.tensor.transpose(by_u[:, u, r * P : (r + 1) * P], words[:, a, r, u, :], ident[:])
                 src = bank[:].rearrange("p (u n) -> p n u", u=2)
-                if half == 0:
-                    nc.vector.tensor_copy(out=dst, in_=src)
+                if a == 0:
+                    nc.vector.tensor_copy(out=pairs[:, a, :, :], in_=src)
                 else:
-                    nc.scalar.copy(out=dst, in_=src)
+                    nc.scalar.copy(out=pairs[:, a, :, :], in_=src)
             count["freed"] += 1
             load_ahead()
 
-        def quantise_x(k_pass):
-            nc.vector.quantize_mx(out=x_codes[:, k_pass, :].bitcast(FP8X4), scales=x_scales[:, k_pass, :],
-                                  in_=x_grouped[k_pass][:])
+        def quantise_x(n):
+            rows = slice((n % 2) * 256, (n % 2 + 1) * 256)
+            for a in range(2):
+                k_pass = 2 * (n // 2) + a
+                nc.vector.quantize_mx(out=x_codes[:, k_pass, rows].bitcast(FP8X4), scales=x_scales[:, k_pass, rows],
+                                      in_=x_grouped[n][:, a * 1024 : (a + 1) * 1024])
+            count["x"] += 1
 
         w_grouped = {}
         w_codes = {}
@@ -231,12 +233,16 @@ def tile_bag_lstm_pa_kernel(tc, x, h_prev, c_prev, is_rnn, W, b, out_0, out_1):
                 )
 
         def multiply_what_is_ready():
-            while count["multiplied"] < count["quantised"] and (
-                count["multiplied"] % PASSES != 0 or count["activated"] >= count["multiplied"] // PASSES
+            while (
+                count["multiplied"] < count["quantised"]
+                and count["x"] >= 2 * (count["multiplied"] % PASSES // 2 + 1)
+                and (count["multiplied"] % PASSES != 0 or count["activated"] >= count["multiplied"] // PASSES)
             ):
                 multiply(count["multiplied"])
                 count["multiplied"] += 1
 
+        c_rows = out_0.rearrange("(p r) c -> p r c", r=ROW_TILES)
+        o_rows = out_1.rearrange("(p r) c -> p r c", r=ROW_TILES)
         acts = {}
         turned = {}
         f_part = {}
@@ -273,7 +279,7 @@ def tile_bag_lstm_pa_kernel(tc, x, h_prev, c_prev, is_rnn, W, b, out_0, out_1):
         def f_times_c(unit):
             half = unit % 2
             nc.vector.tensor_tensor(out=f_part[half][:], in0=f_part[half][:],
-                                    in1=c_sb[:, half, :, :], op=ALU.mult)
+                                    in1=c_sb[:, :, half * UNIT : (half + 1) * UNIT], op=ALU.mult)
 
         def i_times_g(unit):
             g_act = acts[GATES.index("g") * 2 + unit % 2]
@@ -286,24 +292,24 @@ def tile_bag_lstm_pa_kernel(tc, x, h_prev, c_prev, is_rnn, W, b, out_0, out_1):
                 res = out_pool.tile([P, UNIT], F32, name="res", tag="res")
                 nc.vector.scalar_tensor_tensor(out=res[:], in0=turned[(unit, r)][:], scalar=m_of(r),
                                                in1=f_part[half][:, r, :], op0=ALU.mult, op1=ALU.add)
-                nc.sync.dma_start(out=out_0[r * P : (r + 1) * P, half * UNIT : (half + 1) * UNIT], in_=res[:])
+                nc.sync.dma_start(out=c_rows[:, r, half * UNIT : (half + 1) * UNIT], in_=res[:])
 
         def o_out(unit):
             half = unit % 2
             for r in range(ROW_TILES):
                 res = out_pool.tile([P, UNIT], F32, name="res", tag="res")
                 blend(res[:], unit, r)
-                nc.sync.dma_start(out=out_1[r * P : (r + 1) * P, half * UNIT : (half + 1) * UNIT], in_=res[:])
+                nc.sync.dma_start(out=o_rows[:, r, half * UNIT : (half + 1) * UNIT], in_=res[:])
 
         for s in range(SLOTS):
             if s < PIECES:
                 regroup(s)
             if 1 <= s <= PIECES:
                 quantise(s - 1)
-            if 1 <= s <= PASSES:
-                quantise_x(s - 1)
-            if s < PASSES:
-                turn_x(s)
+            for chunk in X_CHUNKS.get(s-1, ()):
+                quantise_x(chunk)
+            for chunk in X_CHUNKS.get(s, ()):
+                turn_x(chunk)
             if s == PASSES:
                 turn_bias_and_m()
             for unit in due(s, LAG_F_BLEND, "f"):

@@ -40,14 +40,17 @@ SHARE_PLAIN = 288
 SHARE_HEAD = 152
 HEAD_SLOTS = PASSES + 1
 X_CHUNKS = {0: (0, 1), 1: (2, 3)}
-RAW_TILES = 22
+PAIRED = "g"
+WIDE_TILES = 6
+NARROW_TILES = 10
+BIAS_SLOT = 1
 
 
 def tile_bag_lstm_pa_kernel(tc, x, h_prev, c_prev, is_rnn, W, b, out_0, out_1):
     nc = tc.nc
     with ExitStack() as ctx:
         const = ctx.enter_context(tc.tile_pool(name="const", bufs=1))
-        raw_pool = ctx.enter_context(tc.tile_pool(name="raw_pool", bufs=RAW_TILES))
+        raw_pool = ctx.enter_context(tc.tile_pool(name="raw_pool", bufs=1))
         grouped_pool = ctx.enter_context(tc.tile_pool(name="grouped_pool", bufs=4))
         code_pool = ctx.enter_context(tc.tile_pool(name="code_pool", bufs=8))
         g_pool = ctx.enter_context(tc.tile_pool(name="g_pool", bufs=2))
@@ -65,7 +68,17 @@ def tile_bag_lstm_pa_kernel(tc, x, h_prev, c_prev, is_rnn, W, b, out_0, out_1):
 
         def due(s, lag, gates=GATES):
             return [u for u in range(UNITS)
-                    if PASSES * u + PASSES - 1 + lag == s and gate_of(u) in gates]
+                    if last_slot(u) + lag == s and gate_of(u) in gates]
+
+        SEQ = []
+        for gi, gate in enumerate(GATES):
+            if gate in PAIRED:
+                SEQ += [(2 * gi + h, k) for k in range(PASSES) for h in range(2)]
+            else:
+                SEQ += [(2 * gi + h, k) for h in range(2) for k in range(PASSES)]
+
+        def last_slot(u):
+            return max(s_ for s_, (u_, k_) in enumerate(SEQ) if u_ == u)
 
         zero = const.tile([P, 1], F32, name="zero", tag="zero")
         warm = const.tile([P, 1], F32, name="warm", tag="warm")
@@ -83,20 +96,24 @@ def tile_bag_lstm_pa_kernel(tc, x, h_prev, c_prev, is_rnn, W, b, out_0, out_1):
         x_raw = {}
         c_sb = const.tile([P, ROW_TILES, H], BF16, name="c_sb", tag="c_sb")
 
-        def load_w(n):
-            unit, k_pass = divmod(n, PASSES)
-            col = BLOCK[gate_of(unit)] * H + (unit % 2) * UNIT
-            tile_ = raw_pool.tile([P, 4, UNIT], BF16, name="w_raw", tag="raw")
-            w_raw[n] = tile_
+        def load_w(key):
+            gate, k_pass = key[0], key[1]
             row = K_PASS * k_pass
-            nc.sync.dma_start(
-                out=tile_[:],
-                in_=W[row : row + K_PASS, col : col + UNIT].rearrange("(q t) c -> q t c", t=4),
-            )
+            wide = len(key) == 2
+            col = BLOCK[gate] * H + (0 if wide else key[2] * UNIT)
+            width = H if wide else UNIT
+            if wide:
+                tile_ = raw_pool.tile([P, 4, H], BF16, name="w_raw", tag="wide", bufs=WIDE_TILES)
+                w_raw[(gate, k_pass, 0)] = tile_[:, :, 0:UNIT]
+                w_raw[(gate, k_pass, 1)] = tile_[:, :, UNIT:H]
+            else:
+                tile_ = raw_pool.tile([P, 4, UNIT], BF16, name="w_raw", tag="raw", bufs=NARROW_TILES)
+                w_raw[key] = tile_
+            nc.sync.dma_start(out=tile_[:], in_=W[row : row + K_PASS, col : col + width].rearrange("(q t) c -> q t c", t=4))
 
         def load_x(n):
             src = (x if n < 2 else h_prev).rearrange("(p r) c -> p r c", r=ROW_TILES)
-            tile_ = raw_pool.tile([P, 2, H], BF16, name="x_raw", tag="raw")
+            tile_ = raw_pool.tile([P, 2, H], BF16, name="x_raw", tag="raw", bufs=NARROW_TILES)
             x_raw[n] = tile_
             nc.sync.dma_start(out=tile_[:], in_=src[:, 2 * (n % 2) : 2 * (n % 2) + 2, :])
 
@@ -105,25 +122,47 @@ def tile_bag_lstm_pa_kernel(tc, x, h_prev, c_prev, is_rnn, W, b, out_0, out_1):
                 out=c_sb[:], in_=c_prev.rearrange("(p r) c -> p r c", r=ROW_TILES),
             )
 
+        def key_of(unit, k_pass):
+            gate = gate_of(unit)
+            if gate in PAIRED and (gate, k_pass) != (GATES[0], 0):
+                return (gate, k_pass)
+            return (gate, k_pass, unit % 2)
+
         load_order = []
         for n in range(PIECES):
-            if due(n + 1, LAG_F_TIMES_C, "f") and ("c",0) not in load_order:
+            unit, k_pass = SEQ[n]
+            gate = gate_of(unit)
+            key = key_of(unit, k_pass)
+            if due(n + 1, LAG_F_TIMES_C, "f") and ("c", 0) not in load_order:
                 load_order.append(("c", 0))
-            load_order.append(("w", n))
+            if ("w", key) not in load_order:
+                load_order.append(("w", key))
             for chunk in X_CHUNKS.get(n, ()):
                 load_order.append(("x", chunk))
+        live = {"wide": [], "raw": []}
+        gone = {}
 
         def load_ahead():
-            while count["loads"] < len(load_order) and count["loads"] - count["freed"] < RAW_TILES:
-                what, n = load_order[count["loads"]]
+            while count["loads"] < len(load_order):
+                item = load_order[count["loads"]]
+                what, n = item
+                if what != "c":
+                    cl = "wide" if what == "w" and len(n) == 2 else "raw"
+                    lim = WIDE_TILES if cl == "wide" else NARROW_TILES
+                    if len(live[cl]) >= lim and gone.get(live[cl][-lim], 0) < (2 if cl == "wide" else 1):
+                        return
+                    live[cl].append(item)
                 if what == "w":
                     load_w(n)
                 elif what == "x":
                     load_x(n)
                 else:
                     load_c()
-                    count["freed"] += 1
                 count["loads"] += 1
+
+        def release(item):
+            gone[item] = gone.get(item, 0) + 1
+            load_ahead()
 
         load_ahead()
 
@@ -164,8 +203,7 @@ def tile_bag_lstm_pa_kernel(tc, x, h_prev, c_prev, is_rnn, W, b, out_0, out_1):
                     nc.vector.tensor_copy(out=pairs[:, a, :, :], in_=src)
                 else:
                     nc.scalar.copy(out=pairs[:, a, :, :], in_=src)
-            count["freed"] += 1
-            load_ahead()
+            release(("x", n))
 
         def quantise_x(n):
             rows = slice((n % 2) * 256, (n % 2 + 1) * 256)
@@ -197,30 +235,32 @@ def tile_bag_lstm_pa_kernel(tc, x, h_prev, c_prev, is_rnn, W, b, out_0, out_1):
             if split > 0:
                 nc.vector.tensor_copy(
                     out=grouped[:, 0:split, :].rearrange("p (c i) t -> p c t i", i=4),
-                    in_=w_raw[n][:, :, 0:split].rearrange("p t (c i) -> p c t i", i=4),
+                    in_=w_raw[(gate_of(SEQ[n][0]), SEQ[n][1], SEQ[n][0] % 2)][:, :, 0:split].rearrange("p t (c i) -> p c t i", i=4),
                 )
             if split < UNIT:
                 nc.scalar.copy(
                     out=grouped[:, split:UNIT, :].rearrange("p (c i) t -> p c t i", i=4),
-                    in_=w_raw[n][:, :, split:UNIT].rearrange("p t (c i) -> p c t i", i=4),
+                    in_=w_raw[(gate_of(SEQ[n][0]), SEQ[n][1], SEQ[n][0] % 2)][:, :, split:UNIT].rearrange("p t (c i) -> p c t i", i=4),
                 )
-            count["freed"] += 1
-            load_ahead()
+            release(("w", key_of(*SEQ[n])))
 
         def quantise(n):
             codes = code_pool.tile([P, UNIT], U32, name="codes", tag="codes", align_bytes=256)
             scales = code_pool.tile([P, UNIT], U8, name="scales", tag="scales", align_bytes=256)
             nc.vector.quantize_mx(out=codes[:].bitcast(FP8X4), scales=scales[:],
                                   in_=w_grouped[n][:].rearrange("p c t -> p (c t)"))
-            w_codes[n] = (codes, scales)
+            w_codes[SEQ[n]] = (codes, scales)
             count["quantised"] += 1
 
-        def multiply(n):
-            unit, k_pass = divmod(n, PASSES)
-            codes, scales = w_codes[n]
+
+        def multiply(unit, k_pass):
+            codes, scales = w_codes[(unit, k_pass)]
+            pool, tag = mx_banks, "mx"
+            if gate_of(unit) in PAIRED and unit % 2:
+                pool, tag = turn_banks, "turn"
             for j in range(TILES):
                 if k_pass == 0:
-                    bank = mx_banks.tile([P, B], F32, name="bank", tag="mx")
+                    bank = pool.tile([P, B], F32, name="bank", tag=tag)
                     banks[(unit, j)] = bank
                 nc.tensor.matmul_mx(
                     out=banks[(unit, j)][:],
@@ -232,13 +272,20 @@ def tile_bag_lstm_pa_kernel(tc, x, h_prev, c_prev, is_rnn, W, b, out_0, out_1):
                     stop=(k_pass == PASSES - 1),
                 )
 
+        acted = set()
+
         def multiply_what_is_ready():
-            while (
-                count["multiplied"] < count["quantised"]
-                and count["x"] >= 2 * (count["multiplied"] % PASSES // 2 + 1)
-                and (count["multiplied"] % PASSES != 0 or count["activated"] >= count["multiplied"] // PASSES)
-            ):
-                multiply(count["multiplied"])
+            while count["multiplied"] < PIECES:
+                unit, k_pass = SEQ[count["multiplied"]]
+                if (unit, k_pass) not in w_codes or count["x"] < 2 * (k_pass // 2 + 1):
+                    return
+                if k_pass == 0:
+                    in_turn = gate_of(unit) in PAIRED and unit % 2
+                    before = [u for u in range(unit) if bool(gate_of(u) in PAIRED and u % 2) == bool(in_turn)]
+                    if before and before[-1] not in acted:
+                        return
+                multiply(unit, k_pass)
+                acted.add((unit, k_pass))
                 count["multiplied"] += 1
 
         c_rows = out_0.rearrange("(p r) c -> p r c", r=ROW_TILES)
@@ -248,6 +295,7 @@ def tile_bag_lstm_pa_kernel(tc, x, h_prev, c_prev, is_rnn, W, b, out_0, out_1):
         f_part = {}
 
         def activate(unit):
+            assert (unit, 3) in acted
             gate = gate_of(unit)
             pool = g_pool if gate == "g" else act_pool
             act = pool.tile([P, TILES, B], F32, name="act", tag="act")
@@ -257,7 +305,7 @@ def tile_bag_lstm_pa_kernel(tc, x, h_prev, c_prev, is_rnn, W, b, out_0, out_1):
                 nc.scalar.activation(out=act[:, j, :], in_=banks[(unit, j)][:],
                                      func=ACT.Tanh if gate == "g" else ACT.Sigmoid,
                                      bias=cols[:, col : col + 1], scale=1.0)
-            count["activated"] += 1
+            acted.add(unit)
 
         def turn_back(unit, src):
             for r in range(ROW_TILES):
@@ -310,7 +358,7 @@ def tile_bag_lstm_pa_kernel(tc, x, h_prev, c_prev, is_rnn, W, b, out_0, out_1):
                 quantise_x(chunk)
             for chunk in X_CHUNKS.get(s, ()):
                 turn_x(chunk)
-            if s == PASSES:
+            if s == BIAS_SLOT:
                 turn_bias_and_m()
             for unit in due(s, LAG_F_BLEND, "f"):
                 f_blend(unit)

@@ -37,13 +37,14 @@ LAG_O_OUT = 5
 SLOTS = PIECES + LAG_O_OUT + 1
 
 SHARE_PLAIN = 288
-SHARE_HEAD = 152
+SHARE_HEAD = 320
 HEAD_SLOTS = PASSES + 1
-X_CHUNKS = {0: (0, 1), 1: (2, 3)}
+RUN = 8
+X_CHUNKS = {0: (0,), 1: (1,), 2: (2, 3)}
 PAIRED = "g"
 WIDE_TILES = 6
 NARROW_TILES = 10
-BIAS_SLOT = 1
+BIAS_SLOT = 2
 
 
 def tile_bag_lstm_pa_kernel(tc, x, h_prev, c_prev, is_rnn, W, b, out_0, out_1):
@@ -170,15 +171,16 @@ def tile_bag_lstm_pa_kernel(tc, x, h_prev, c_prev, is_rnn, W, b, out_0, out_1):
         m_cols = const.tile([P, ROW_TILES], F32, name="m_cols", tag="m_cols")
         one_minus_m = const.tile([P, ROW_TILES], F32, name="one_minus_m", tag="one_minus_m")
 
-        def turn_bias_and_m():
-            rows_f32 = const.tile([P, P], F32, name="rows_f32", tag="rows_f32")
-            nc.vector.tensor_copy(out=rows_f32[:], in_=rows_bf[:])
+        rows_f32 = const.tile([P, P], F32, name="rows_f32", tag="rows_f32")
+        nc.gpsimd.tensor_copy(out=rows_f32[:], in_=rows_bf[:])
+        nc.gpsimd.tensor_copy(out=m_cols[:], in_=m_bf[:])
+        nc.gpsimd.tensor_scalar(out=one_minus_m[:], in0=m_cols[:], scalar1=-1.0, scalar2=1.0,
+                                op0=ALU.mult, op1=ALU.add)
+
+        def turn_bias():
             bank = turn_banks.tile([P, 512], F32, name="bank", tag="turn")
             nc.tensor.transpose(bank[:, 0:P], rows_f32[:], ident[:])
-            nc.vector.tensor_copy(out=cols[:], in_=bank[:, 0:32])
-            nc.vector.tensor_copy(out=m_cols[:], in_=m_bf[:])
-            nc.vector.tensor_scalar(out=one_minus_m[:], in0=m_cols[:], scalar1=-1.0, scalar2=1.0,
-                                    op0=ALU.mult, op1=ALU.add)
+            nc.scalar.copy(out=cols[:], in_=bank[:, 0:32])
 
         def m_of(r):
             return m_cols[:, r : r + 1]
@@ -199,10 +201,7 @@ def tile_bag_lstm_pa_kernel(tc, x, h_prev, c_prev, is_rnn, W, b, out_0, out_1):
                     for r in range(2):
                         nc.tensor.transpose(by_u[:, u, r * P : (r + 1) * P], words[:, a, r, u, :], ident[:])
                 src = bank[:].rearrange("p (u n) -> p n u", u=2)
-                if a == 0:
-                    nc.vector.tensor_copy(out=pairs[:, a, :, :], in_=src)
-                else:
-                    nc.scalar.copy(out=pairs[:, a, :, :], in_=src)
+                nc.scalar.copy(out=pairs[:, a, :, :], in_=src)
             release(("x", n))
 
         def quantise_x(n):
@@ -234,13 +233,13 @@ def tile_bag_lstm_pa_kernel(tc, x, h_prev, c_prev, is_rnn, W, b, out_0, out_1):
             split = vector_share(n)
             if split > 0:
                 nc.vector.tensor_copy(
-                    out=grouped[:, 0:split, :].rearrange("p (c i) t -> p c t i", i=4),
-                    in_=w_raw[(gate_of(SEQ[n][0]), SEQ[n][1], SEQ[n][0] % 2)][:, :, 0:split].rearrange("p t (c i) -> p c t i", i=4),
+                    out=grouped[:, 0:split, :].rearrange("p (c i) t -> p c t i", i=RUN),
+                    in_=w_raw[(gate_of(SEQ[n][0]), SEQ[n][1], SEQ[n][0] % 2)][:, :, 0:split].rearrange("p t (c i) -> p c t i", i=RUN),
                 )
             if split < UNIT:
                 nc.scalar.copy(
-                    out=grouped[:, split:UNIT, :].rearrange("p (c i) t -> p c t i", i=4),
-                    in_=w_raw[(gate_of(SEQ[n][0]), SEQ[n][1], SEQ[n][0] % 2)][:, :, split:UNIT].rearrange("p t (c i) -> p c t i", i=4),
+                    out=grouped[:, split:UNIT, :].rearrange("p (c i) t -> p c t i", i=RUN),
+                    in_=w_raw[(gate_of(SEQ[n][0]), SEQ[n][1], SEQ[n][0] % 2)][:, :, split:UNIT].rearrange("p t (c i) -> p c t i", i=RUN),
                 )
             release(("w", key_of(*SEQ[n])))
 
@@ -359,7 +358,7 @@ def tile_bag_lstm_pa_kernel(tc, x, h_prev, c_prev, is_rnn, W, b, out_0, out_1):
             for chunk in X_CHUNKS.get(s, ()):
                 turn_x(chunk)
             if s == BIAS_SLOT:
-                turn_bias_and_m()
+                turn_bias()
             for unit in due(s, LAG_F_BLEND, "f"):
                 f_blend(unit)
             for unit in due(s, LAG_F_TIMES_C, "f"):

@@ -31,7 +31,7 @@ LAG_ACTIVATE = 3
 LAG_TRANSPOSE = 4
 LAG_F_BLEND = 6
 LAG_F_TIMES_C = 8
-LAG_I_TIMES_G = 10
+LAG_I_TIMES_G = (8, 9)
 LAG_C_OUT = 11
 LAG_O_OUT = 5
 SLOTS = PIECES + LAG_O_OUT + 1
@@ -41,9 +41,9 @@ SHARE_HEAD = 320
 HEAD_SLOTS = PASSES + 1
 RUN = 8
 X_CHUNKS = {0: (0,), 1: (1,), 2: (2, 3)}
-PAIRED = "g"
+PAIRED = ""
 WIDE_TILES = 6
-NARROW_TILES = 10
+NARROW_TILES = 22
 BIAS_SLOT = 2
 
 
@@ -70,6 +70,9 @@ def tile_bag_lstm_pa_kernel(tc, x, h_prev, c_prev, is_rnn, W, b, out_0, out_1):
         def due(s, lag, gates=GATES):
             return [u for u in range(UNITS)
                     if last_slot(u) + lag == s and gate_of(u) in gates]
+
+        def due_i_times_g(s):
+            return [u for half in range(2) for u in due(s, LAG_I_TIMES_G[half], "i") if u % 2 == half]
 
         SEQ = []
         for gi, gate in enumerate(GATES):
@@ -118,10 +121,9 @@ def tile_bag_lstm_pa_kernel(tc, x, h_prev, c_prev, is_rnn, W, b, out_0, out_1):
             x_raw[n] = tile_
             nc.sync.dma_start(out=tile_[:], in_=src[:, 2 * (n % 2) : 2 * (n % 2) + 2, :])
 
-        def load_c():
-            nc.sync.dma_start(
-                out=c_sb[:], in_=c_prev.rearrange("(p r) c -> p r c", r=ROW_TILES),
-            )
+        def load_c(half):
+            cs = slice(half * UNIT, (half + 1) * UNIT)
+            nc.sync.dma_start(out=c_sb[:, :, cs], in_=c_prev.rearrange("(p r) c -> p r c", r=ROW_TILES)[:, :, cs])
 
         def key_of(unit, k_pass):
             gate = gate_of(unit)
@@ -134,8 +136,8 @@ def tile_bag_lstm_pa_kernel(tc, x, h_prev, c_prev, is_rnn, W, b, out_0, out_1):
             unit, k_pass = SEQ[n]
             gate = gate_of(unit)
             key = key_of(unit, k_pass)
-            if due(n + 1, LAG_F_TIMES_C, "f") and ("c", 0) not in load_order:
-                load_order.append(("c", 0))
+            for unit_f in due(n + 1, LAG_F_TIMES_C, "f"):
+                load_order.append(("c", unit_f % 2))
             if ("w", key) not in load_order:
                 load_order.append(("w", key))
             for chunk in X_CHUNKS.get(n, ()):
@@ -158,7 +160,7 @@ def tile_bag_lstm_pa_kernel(tc, x, h_prev, c_prev, is_rnn, W, b, out_0, out_1):
                 elif what == "x":
                     load_x(n)
                 else:
-                    load_c()
+                    load_c(n)
                 count["loads"] += 1
 
         def release(item):
@@ -220,7 +222,7 @@ def tile_bag_lstm_pa_kernel(tc, x, h_prev, c_prev, is_rnn, W, b, out_0, out_1):
             if s < HEAD_SLOTS:
                 return SHARE_HEAD
             scalar_busy = due(s, LAG_ACTIVATE) or due(s, LAG_F_BLEND, "f") or due(s, LAG_O_OUT, "o")
-            vector_busy = due(s, LAG_F_TIMES_C, "f") or due(s, LAG_I_TIMES_G, "i") or due(s, LAG_C_OUT, "i")
+            vector_busy = due(s, LAG_F_TIMES_C, "f") or due_i_times_g(s) or due(s, LAG_C_OUT, "i")
             if scalar_busy and not vector_busy:
                 return UNIT
             if vector_busy and not scalar_busy:
@@ -252,40 +254,45 @@ def tile_bag_lstm_pa_kernel(tc, x, h_prev, c_prev, is_rnn, W, b, out_0, out_1):
             count["quantised"] += 1
 
 
-        def multiply(unit, k_pass):
+        def one_pass(unit, k_pass, j):
             codes, scales = w_codes[(unit, k_pass)]
             pool, tag = mx_banks, "mx"
             if gate_of(unit) in PAIRED and unit % 2:
                 pool, tag = turn_banks, "turn"
-            for j in range(TILES):
-                if k_pass == 0:
-                    bank = pool.tile([P, B], F32, name="bank", tag=tag)
-                    banks[(unit, j)] = bank
-                nc.tensor.matmul_mx(
-                    out=banks[(unit, j)][:],
-                    lhsT=codes[:, j * P : (j + 1) * P].bitcast(FP8X4),
-                    lhsT_scale=scales[:, j * P : (j + 1) * P],
-                    rhs=x_codes[:, k_pass, :].bitcast(FP8X4),
-                    rhs_scale=x_scales[:, k_pass, :],
-                    start=(k_pass == 0),
-                    stop=(k_pass == PASSES - 1),
-                )
+            if k_pass == 0:
+                bank = pool.tile([P, B], F32, name="bank", tag=tag)
+                banks[(unit, j)] = bank
+            nc.tensor.matmul_mx(
+                out=banks[(unit, j)][:],
+                lhsT=codes[:, j * P : (j + 1) * P].bitcast(FP8X4),
+                lhsT_scale=scales[:, j * P : (j + 1) * P],
+                rhs=x_codes[:, k_pass, :].bitcast(FP8X4),
+                rhs_scale=x_scales[:, k_pass, :],
+                start=(k_pass == 0),
+                stop=(k_pass == PASSES - 1),
+            )
 
         acted = set()
 
         def multiply_what_is_ready():
+            ready = []
             while count["multiplied"] < PIECES:
                 unit, k_pass = SEQ[count["multiplied"]]
                 if (unit, k_pass) not in w_codes or count["x"] < 2 * (k_pass // 2 + 1):
-                    return
+                    break
                 if k_pass == 0:
                     in_turn = gate_of(unit) in PAIRED and unit % 2
                     before = [u for u in range(unit) if bool(gate_of(u) in PAIRED and u % 2) == bool(in_turn)]
                     if before and before[-1] not in acted:
-                        return
-                multiply(unit, k_pass)
+                        break
+                ready.append((unit, k_pass))
                 acted.add((unit, k_pass))
                 count["multiplied"] += 1
+            for unit in sorted(set(unit for unit, k_pass in ready)):
+                for pair in range(TILES // 2):
+                    for k_pass in [k for u, k in ready if u == unit]:
+                        for j in (2 * pair, 2 * pair + 1):
+                            one_pass(unit, k_pass, j)
 
         c_rows = out_0.rearrange("(p r) c -> p r c", r=ROW_TILES)
         o_rows = out_1.rearrange("(p r) c -> p r c", r=ROW_TILES)
@@ -363,7 +370,7 @@ def tile_bag_lstm_pa_kernel(tc, x, h_prev, c_prev, is_rnn, W, b, out_0, out_1):
                 f_blend(unit)
             for unit in due(s, LAG_F_TIMES_C, "f"):
                 f_times_c(unit)
-            for unit in due(s, LAG_I_TIMES_G, "i"):
+            for unit in due_i_times_g(s):
                 i_times_g(unit)
             for unit in due(s, LAG_C_OUT, "i"):
                 c_out(unit)

@@ -22,7 +22,7 @@ PASSES = K // K_PASS
 ROW_TILES = B // P
 UNIT = 512
 TILES = UNIT // P
-GATES = "gfio"
+GATES = "fgio"
 BLOCK = {"i": 0, "f": 1, "g": 2, "o": 3}
 UNITS = 2 * len(GATES)
 PIECES = UNITS * PASSES
@@ -36,11 +36,11 @@ LAG_C_OUT = 11
 LAG_O_OUT = 5
 SLOTS = PIECES + LAG_O_OUT + 1
 
-SHARE_PLAIN = 288
-SHARE_HEAD = 320
+SHARE_PLAIN = 272
+SHARE_HEAD = 256
 HEAD_SLOTS = PASSES + 1
 RUN = 8
-X_CHUNKS = {0: (0,), 1: (1,), 2: (2, 3)}
+X_CHUNKS = {0: (0, 1), 1: (2, 3)}
 PAIRED = ""
 WIDE_TILES = 6
 NARROW_TILES = 22

@@ -32,11 +32,12 @@ LAG_TRANSPOSE = 4
 LAG_F_BLEND = 6
 LAG_F_TIMES_C = 8
 LAG_I_TIMES_G = (8, 9)
+I_TIMES_G_PARTS = (1, 2)
 LAG_C_OUT = 11
 LAG_O_OUT = 5
 SLOTS = PIECES + LAG_O_OUT + 1
 
-SHARE_PLAIN = 272
+SHARE_PLAIN = 288
 SHARE_HEAD = 256
 HEAD_SLOTS = PASSES + 1
 RUN = 8
@@ -193,25 +194,23 @@ def tile_bag_lstm_pa_kernel(tc, x, h_prev, c_prev, is_rnn, W, b, out_0, out_1):
 
         def turn_x(n):
             words = x_raw[n][:].rearrange("p r c -> p (r c)").bitcast(F32).rearrange("p (r a q u) -> p a r u q", r=2, a=2, u=2)
-            grouped = grouped_pool.tile([P, 4 * B], BF16, name="x_grouped", tag="grouped", align_bytes=256)
-            x_grouped[n] = grouped
-            pairs = grouped[:].bitcast(F32).rearrange("p (a n u) -> p a n u", a=2, u=2)
             for a in range(2):
+                k_pass = 2 * (n // 2) + a
+                if n % 2 == 0:
+                    grouped = grouped_pool.tile([P, 4 * B], BF16, name="x_grouped", tag="grouped", align_bytes=256)
+                    x_grouped[k_pass] = grouped
                 bank = turn_banks.tile([P, 512], F32, name="bank", tag="turn")
                 by_u = bank[:].rearrange("p (u n) -> p u n", u=2)
                 for u in range(2):
                     for r in range(2):
                         nc.tensor.transpose(by_u[:, u, r * P : (r + 1) * P], words[:, a, r, u, :], ident[:])
-                src = bank[:].rearrange("p (u n) -> p n u", u=2)
-                nc.scalar.copy(out=pairs[:, a, :, :], in_=src)
+                pairs = x_grouped[k_pass][:].bitcast(F32).rearrange("p (n u) -> p n u", u=2)
+                nc.scalar.copy(out=pairs[:, (n % 2) * 256 : (n % 2 + 1) * 256, :], in_=bank[:].rearrange("p (u n) -> p n u", u=2))
             release(("x", n))
 
-        def quantise_x(n):
-            rows = slice((n % 2) * 256, (n % 2 + 1) * 256)
-            for a in range(2):
-                k_pass = 2 * (n // 2) + a
-                nc.vector.quantize_mx(out=x_codes[:, k_pass, rows].bitcast(FP8X4), scales=x_scales[:, k_pass, rows],
-                                      in_=x_grouped[n][:, a * 1024 : (a + 1) * 1024])
+        def quantise_x(k_pass):
+            nc.vector.quantize_mx(out=x_codes[:, k_pass, :].bitcast(FP8X4), scales=x_scales[:, k_pass, :],
+                                  in_=x_grouped[k_pass][:])
             count["x"] += 1
 
         w_grouped = {}
@@ -278,7 +277,7 @@ def tile_bag_lstm_pa_kernel(tc, x, h_prev, c_prev, is_rnn, W, b, out_0, out_1):
             ready = []
             while count["multiplied"] < PIECES:
                 unit, k_pass = SEQ[count["multiplied"]]
-                if (unit, k_pass) not in w_codes or count["x"] < 2 * (k_pass // 2 + 1):
+                if (unit, k_pass) not in w_codes or count["x"] <= k_pass:
                     break
                 if k_pass == 0:
                     in_turn = gate_of(unit) in PAIRED and unit % 2
@@ -337,7 +336,10 @@ def tile_bag_lstm_pa_kernel(tc, x, h_prev, c_prev, is_rnn, W, b, out_0, out_1):
 
         def i_times_g(unit):
             g_act = acts[GATES.index("g") * 2 + unit % 2]
-            nc.vector.tensor_tensor(out=g_act[:], in0=acts[unit][:], in1=g_act[:], op=ALU.mult)
+            parts = I_TIMES_G_PARTS[unit % 2]
+            for n in range(parts):
+                rows = slice(n * B // parts, (n + 1) * B // parts)
+                nc.vector.tensor_tensor(out=g_act[:, :, rows], in0=acts[unit][:, :, rows], in1=g_act[:, :, rows], op=ALU.mult)
 
         def c_out(unit):
             half = unit % 2

from contextlib import ExitStack

import concourse.mybir as mybir
from concourse.masks import make_identity

F32 = mybir.dt.float32
BF16 = mybir.dt.bfloat16
U32 = mybir.dt.uint32
U8 = mybir.dt.uint8
FP8X4 = mybir.dt.float8_e4m3fn_x4
ACT = mybir.ActivationFunctionType
ALU = mybir.AluOpType

P = 128
B = 512
H = 1024
K = 2 * H
FLOPS = 2 * B * K * 4 * H

K_PASS = 512
PASSES = K // K_PASS
ROW_TILES = B // P
UNIT = 512
TILES = UNIT // P
GATES = "fgio"
BLOCK = {"i": 0, "f": 1, "g": 2, "o": 3}
UNITS = 2 * len(GATES)
PIECES = UNITS * PASSES

LAG_ACTIVATE = 3
LAG_TRANSPOSE = 4
LAG_F_BLEND = 6
LAG_F_TIMES_C = 8
LAG_I_TIMES_G = (8, 9)
I_TIMES_G_PARTS = (1, 2)
LAG_C_OUT = 11
LAG_O_OUT = 5
SLOTS = PIECES + LAG_O_OUT + 1

SHARE_PLAIN = 288
SHARE_HEAD = 256
HEAD_SLOTS = PASSES + 1
RUN = 8
X_CHUNKS = {0: (0, 1), 1: (2, 3)}
PAIRED = ""
WIDE_TILES = 6
NARROW_TILES = 22
BIAS_SLOT = 2


def tile_bag_lstm_pa_kernel(tc, x, h_prev, c_prev, is_rnn, W, b, out_0, out_1):
    nc = tc.nc
    with ExitStack() as ctx:
        const = ctx.enter_context(tc.tile_pool(name="const", bufs=1))
        raw_pool = ctx.enter_context(tc.tile_pool(name="raw_pool", bufs=1))
        grouped_pool = ctx.enter_context(tc.tile_pool(name="grouped_pool", bufs=4))
        code_pool = ctx.enter_context(tc.tile_pool(name="code_pool", bufs=8))
        g_pool = ctx.enter_context(tc.tile_pool(name="g_pool", bufs=2))
        act_pool = ctx.enter_context(tc.tile_pool(name="act_pool", bufs=3))
        f_pool = ctx.enter_context(tc.tile_pool(name="f_pool", bufs=2))
        out_pool = ctx.enter_context(tc.tile_pool(name="out_pool", bufs=10))
        mx_banks = ctx.enter_context(tc.psum_pool(name="mx_banks", bufs=TILES))
        turn_banks = ctx.enter_context(tc.psum_pool(name="turn_banks", bufs=ROW_TILES))
        ctx.enter_context(tc.manual_schedule())

        count = {"loads": 0, "freed": 0, "quantised": 0, "multiplied": 0, "activated": 0, "x": 0}

        def gate_of(unit):
            return GATES[unit // 2]

        def due(s, lag, gates=GATES):
            return [u for u in range(UNITS)
                    if last_slot(u) + lag == s and gate_of(u) in gates]

        def due_i_times_g(s):
            return [u for half in range(2) for u in due(s, LAG_I_TIMES_G[half], "i") if u % 2 == half]

        SEQ = []
        for gi, gate in enumerate(GATES):
            if gate in PAIRED:
                SEQ += [(2 * gi + h, k) for k in range(PASSES) for h in range(2)]
            else:
                SEQ += [(2 * gi + h, k) for h in range(2) for k in range(PASSES)]

        def last_slot(u):
            return max(s_ for s_, (u_, k_) in enumerate(SEQ) if u_ == u)

        zero = const.tile([P, 1], F32, name="zero", tag="zero")
        warm = const.tile([P, 1], F32, name="warm", tag="warm")
        nc.vector.memset(zero[:], 0.0)
        rows_bf = const.tile([P, P], BF16, name="rows_bf", tag="rows_bf")
        nc.vector.memset(rows_bf[:], 0.0)
        nc.scalar.dma_start(out=rows_bf[0:32, :], in_=b.rearrange("(r c) -> r c", c=P))
        m_bf = const.tile([P, ROW_TILES], BF16, name="m_bf", tag="m_bf")
        nc.scalar.dma_start(out=m_bf[:], in_=is_rnn.rearrange("(p r) o -> p (r o)", r=ROW_TILES))
        nc.scalar.activation(out=warm[:], in_=zero[:], func=ACT.Sigmoid)
        ident = const.tile([P, P], F32, name="ident", tag="ident")
        make_identity(nc, ident[:])

        w_raw = {}
        x_raw = {}
        c_sb = const.tile([P, ROW_TILES, H], BF16, name="c_sb", tag="c_sb")

        def load_w(key):
            gate, k_pass = key[0], key[1]
            row = K_PASS * k_pass
            wide = len(key) == 2
            col = BLOCK[gate] * H + (0 if wide else key[2] * UNIT)
            width = H if wide else UNIT
            if wide:
                tile_ = raw_pool.tile([P, 4, H], BF16, name="w_raw", tag="wide", bufs=WIDE_TILES)
                w_raw[(gate, k_pass, 0)] = tile_[:, :, 0:UNIT]
                w_raw[(gate, k_pass, 1)] = tile_[:, :, UNIT:H]
            else:
                tile_ = raw_pool.tile([P, 4, UNIT], BF16, name="w_raw", tag="raw", bufs=NARROW_TILES)
                w_raw[key] = tile_
            nc.sync.dma_start(out=tile_[:], in_=W[row : row + K_PASS, col : col + width].rearrange("(q t) c -> q t c", t=4))

        def load_x(n):
            src = (x if n < 2 else h_prev).rearrange("(p r) c -> p r c", r=ROW_TILES)
            tile_ = raw_pool.tile([P, 2, H], BF16, name="x_raw", tag="raw", bufs=NARROW_TILES)
            x_raw[n] = tile_
            nc.sync.dma_start(out=tile_[:], in_=src[:, 2 * (n % 2) : 2 * (n % 2) + 2, :])

        def load_c(half):
            cs = slice(half * UNIT, (half + 1) * UNIT)
            nc.sync.dma_start(out=c_sb[:, :, cs], in_=c_prev.rearrange("(p r) c -> p r c", r=ROW_TILES)[:, :, cs])

        def key_of(unit, k_pass):
            gate = gate_of(unit)
            if gate in PAIRED and (gate, k_pass) != (GATES[0], 0):
                return (gate, k_pass)
            return (gate, k_pass, unit % 2)

        load_order = []
        for n in range(PIECES):
            unit, k_pass = SEQ[n]
            gate = gate_of(unit)
            key = key_of(unit, k_pass)
            for unit_f in due(n + 1, LAG_F_TIMES_C, "f"):
                load_order.append(("c", unit_f % 2))
            if ("w", key) not in load_order:
                load_order.append(("w", key))
            for chunk in X_CHUNKS.get(n, ()):
                load_order.append(("x", chunk))
        live = {"wide": [], "raw": []}
        gone = {}

        def load_ahead():
            while count["loads"] < len(load_order):
                item = load_order[count["loads"]]
                what, n = item
                if what != "c":
                    cl = "wide" if what == "w" and len(n) == 2 else "raw"
                    lim = WIDE_TILES if cl == "wide" else NARROW_TILES
                    if len(live[cl]) >= lim and gone.get(live[cl][-lim], 0) < (2 if cl == "wide" else 1):
                        return
                    live[cl].append(item)
                if what == "w":
                    load_w(n)
                elif what == "x":
                    load_x(n)
                else:
                    load_c(n)
                count["loads"] += 1

        def release(item):
            gone[item] = gone.get(item, 0) + 1
            load_ahead()

        load_ahead()

        cols = const.tile([P, 32], F32, name="cols", tag="cols")
        m_cols = const.tile([P, ROW_TILES], F32, name="m_cols", tag="m_cols")
        one_minus_m = const.tile([P, ROW_TILES], F32, name="one_minus_m", tag="one_minus_m")

        rows_f32 = const.tile([P, P], F32, name="rows_f32", tag="rows_f32")
        nc.gpsimd.tensor_copy(out=rows_f32[:], in_=rows_bf[:])
        nc.gpsimd.tensor_copy(out=m_cols[:], in_=m_bf[:])
        nc.gpsimd.tensor_scalar(out=one_minus_m[:], in0=m_cols[:], scalar1=-1.0, scalar2=1.0,
                                op0=ALU.mult, op1=ALU.add)

        def turn_bias():
            bank = turn_banks.tile([P, 512], F32, name="bank", tag="turn")
            nc.tensor.transpose(bank[:, 0:P], rows_f32[:], ident[:])
            nc.scalar.copy(out=cols[:], in_=bank[:, 0:32])

        def m_of(r):
            return m_cols[:, r : r + 1]

        x_codes = const.tile([P, PASSES, B], U32, name="x_codes", tag="x_codes", align_bytes=256)
        x_scales = const.tile([P, PASSES, B], U8, name="x_scales", tag="x_scales", align_bytes=256)
        x_grouped = {}

        def turn_x(n):
            words = x_raw[n][:].rearrange("p r c -> p (r c)").bitcast(F32).rearrange("p (r a q u) -> p a r u q", r=2, a=2, u=2)
            for a in range(2):
                k_pass = 2 * (n // 2) + a
                if n % 2 == 0:
                    grouped = grouped_pool.tile([P, 4 * B], BF16, name="x_grouped", tag="grouped", align_bytes=256)
                    x_grouped[k_pass] = grouped
                bank = turn_banks.tile([P, 512], F32, name="bank", tag="turn")
                by_u = bank[:].rearrange("p (u n) -> p u n", u=2)
                for u in range(2):
                    for r in range(2):
                        nc.tensor.transpose(by_u[:, u, r * P : (r + 1) * P], words[:, a, r, u, :], ident[:])
                pairs = x_grouped[k_pass][:].bitcast(F32).rearrange("p (n u) -> p n u", u=2)
                nc.scalar.copy(out=pairs[:, (n % 2) * 256 : (n % 2 + 1) * 256, :], in_=bank[:].rearrange("p (u n) -> p n u", u=2))
            release(("x", n))

        def quantise_x(k_pass):
            nc.vector.quantize_mx(out=x_codes[:, k_pass, :].bitcast(FP8X4), scales=x_scales[:, k_pass, :],
                                  in_=x_grouped[k_pass][:])
            count["x"] += 1

        w_grouped = {}
        w_codes = {}
        banks = {}

        def vector_share(s):
            if s < HEAD_SLOTS:
                return SHARE_HEAD
            scalar_busy = due(s, LAG_ACTIVATE) or due(s, LAG_F_BLEND, "f") or due(s, LAG_O_OUT, "o")
            vector_busy = due(s, LAG_F_TIMES_C, "f") or due_i_times_g(s) or due(s, LAG_C_OUT, "i")
            if scalar_busy and not vector_busy:
                return UNIT
            if vector_busy and not scalar_busy:
                return 0
            return SHARE_PLAIN

        def regroup(n):
            grouped = grouped_pool.tile([P, UNIT, 4], BF16, name="w_grouped", tag="grouped", align_bytes=256)
            w_grouped[n] = grouped
            split = vector_share(n)
            if split > 0:
                nc.vector.tensor_copy(
                    out=grouped[:, 0:split, :].rearrange("p (c i) t -> p c t i", i=RUN),
                    in_=w_raw[(gate_of(SEQ[n][0]), SEQ[n][1], SEQ[n][0] % 2)][:, :, 0:split].rearrange("p t (c i) -> p c t i", i=RUN),
                )
            if split < UNIT:
                nc.scalar.copy(
                    out=grouped[:, split:UNIT, :].rearrange("p (c i) t -> p c t i", i=RUN),
                    in_=w_raw[(gate_of(SEQ[n][0]), SEQ[n][1], SEQ[n][0] % 2)][:, :, split:UNIT].rearrange("p t (c i) -> p c t i", i=RUN),
                )
            release(("w", key_of(*SEQ[n])))

        def quantise(n):
            codes = code_pool.tile([P, UNIT], U32, name="codes", tag="codes", align_bytes=256)
            scales = code_pool.tile([P, UNIT], U8, name="scales", tag="scales", align_bytes=256)
            nc.vector.quantize_mx(out=codes[:].bitcast(FP8X4), scales=scales[:],
                                  in_=w_grouped[n][:].rearrange("p c t -> p (c t)"))
            w_codes[SEQ[n]] = (codes, scales)
            count["quantised"] += 1


        def one_pass(unit, k_pass, j):
            codes, scales = w_codes[(unit, k_pass)]
            pool, tag = mx_banks, "mx"
            if gate_of(unit) in PAIRED and unit % 2:
                pool, tag = turn_banks, "turn"
            if k_pass == 0:
                bank = pool.tile([P, B], F32, name="bank", tag=tag)
                banks[(unit, j)] = bank
            nc.tensor.matmul_mx(
                out=banks[(unit, j)][:],
                lhsT=codes[:, j * P : (j + 1) * P].bitcast(FP8X4),
                lhsT_scale=scales[:, j * P : (j + 1) * P],
                rhs=x_codes[:, k_pass, :].bitcast(FP8X4),
                rhs_scale=x_scales[:, k_pass, :],
                start=(k_pass == 0),
                stop=(k_pass == PASSES - 1),
            )

        acted = set()

        def multiply_what_is_ready():
            ready = []
            while count["multiplied"] < PIECES:
                unit, k_pass = SEQ[count["multiplied"]]
                if (unit, k_pass) not in w_codes or count["x"] <= k_pass:
                    break
                if k_pass == 0:
                    in_turn = gate_of(unit) in PAIRED and unit % 2
                    before = [u for u in range(unit) if bool(gate_of(u) in PAIRED and u % 2) == bool(in_turn)]
                    if before and before[-1] not in acted:
                        break
                ready.append((unit, k_pass))
                acted.add((unit, k_pass))
                count["multiplied"] += 1
            for unit in sorted(set(unit for unit, k_pass in ready)):
                for pair in range(TILES // 2):
                    for k_pass in [k for u, k in ready if u == unit]:
                        for j in (2 * pair, 2 * pair + 1):
                            one_pass(unit, k_pass, j)

        c_rows = out_0.rearrange("(p r) c -> p r c", r=ROW_TILES)
        o_rows = out_1.rearrange("(p r) c -> p r c", r=ROW_TILES)
        acts = {}
        turned = {}
        f_part = {}

        def activate(unit):
            assert (unit, 3) in acted
            gate = gate_of(unit)
            pool = g_pool if gate == "g" else act_pool
            act = pool.tile([P, TILES, B], F32, name="act", tag="act")
            acts[unit] = act
            for j in range(TILES):
                col = BLOCK[gate] * (H // P) + (unit % 2) * TILES + j
                nc.scalar.activation(out=act[:, j, :], in_=banks[(unit, j)][:],
                                     func=ACT.Tanh if gate == "g" else ACT.Sigmoid,
                                     bias=cols[:, col : col + 1], scale=1.0)
            acted.add(unit)

        def turn_back(unit, src):
            for r in range(ROW_TILES):
                bank = turn_banks.tile([P, UNIT], F32, name="bank", tag="turn")
                turned[(unit, r)] = bank
                for j in range(TILES):
                    nc.tensor.transpose(bank[:, j * P : (j + 1) * P], src[:, j, r * P : (r + 1) * P], ident[:])

        def blend(dst, unit, r):
            nc.scalar.activation(out=dst, in_=turned[(unit, r)][:], func=ACT.Identity,
                                 bias=one_minus_m[:, r : r + 1], scale=m_of(r))

        def f_blend(unit):
            part = f_pool.tile([P, ROW_TILES, UNIT], F32, name="part", tag="part")
            f_part[unit % 2] = part
            for r in range(ROW_TILES):
                blend(part[:, r, :], unit, r)

        def f_times_c(unit):
            half = unit % 2
            nc.vector.tensor_tensor(out=f_part[half][:], in0=f_part[half][:],
                                    in1=c_sb[:, :, half * UNIT : (half + 1) * UNIT], op=ALU.mult)

        def i_times_g(unit):
            g_act = acts[GATES.index("g") * 2 + unit % 2]
            parts = I_TIMES_G_PARTS[unit % 2]
            for n in range(parts):
                rows = slice(n * B // parts, (n + 1) * B // parts)
                nc.vector.tensor_tensor(out=g_act[:, :, rows], in0=acts[unit][:, :, rows], in1=g_act[:, :, rows], op=ALU.mult)

        def c_out(unit):
            half = unit % 2
            turn_back(unit, acts[GATES.index("g") * 2 + half])
            for r in range(ROW_TILES):
                res = out_pool.tile([P, UNIT], F32, name="res", tag="res")
                nc.vector.scalar_tensor_tensor(out=res[:], in0=turned[(unit, r)][:], scalar=m_of(r),
                                               in1=f_part[half][:, r, :], op0=ALU.mult, op1=ALU.add)
                nc.sync.dma_start(out=c_rows[:, r, half * UNIT : (half + 1) * UNIT], in_=res[:])

        def o_out(unit):
            half = unit % 2
            for r in range(ROW_TILES):
                res = out_pool.tile([P, UNIT], F32, name="res", tag="res")
                blend(res[:], unit, r)
                nc.sync.dma_start(out=o_rows[:, r, half * UNIT : (half + 1) * UNIT], in_=res[:])

        for s in range(SLOTS):
            if s < PIECES:
                regroup(s)
            if 1 <= s <= PIECES:
                quantise(s - 1)
            for chunk in X_CHUNKS.get(s-1, ()):
                quantise_x(chunk)
            for chunk in X_CHUNKS.get(s, ()):
                turn_x(chunk)
            if s == BIAS_SLOT:
                turn_bias()
            for unit in due(s, LAG_F_BLEND, "f"):
                f_blend(unit)
            for unit in due(s, LAG_F_TIMES_C, "f"):
                f_times_c(unit)
            for unit in due_i_times_g(s):
                i_times_g(unit)
            for unit in due(s, LAG_C_OUT, "i"):
                c_out(unit)
            for unit in due(s, LAG_O_OUT, "o"):
                o_out(unit)
            for unit in due(s, LAG_ACTIVATE):
                activate(unit)
            for unit in due(s, LAG_TRANSPOSE, "fo"):
                turn_back(unit, acts[unit])
            multiply_what_is_ready()
